import numpy as np
import ml_dtypes


def mxq(x, axis, fmt="e4m3"):
    dtype, down = {"e4m3": (ml_dtypes.float8_e4m3fn, 7), "e5m2": (ml_dtypes.float8_e5m2, 14)}[fmt]
    v = np.moveaxis(np.asarray(x, np.float32).astype(ml_dtypes.bfloat16).astype(np.float64), axis, -1)
    blocks = v.reshape(v.shape[:-1] + (-1, 32))
    amax = np.abs(blocks).max(-1, keepdims=True)
    byte = np.maximum(np.where(amax > 0, np.frexp(amax)[1] - 1 + 127, 0) - down, 1)
    scale = np.exp2(byte - 127.0)
    codes = (blocks / scale).astype(np.float32).astype(dtype).astype(np.float64)
    return np.moveaxis((codes * scale).reshape(v.shape), -1, axis)


WIDE = False


def mx_kscale(k):
    if not WIDE:
        return np.ones(k)
    levels = np.array([10, -10, 5, -5, 0])
    if k % 512:
        return np.exp2(np.random.permutation(np.resize(levels, k // 32))).repeat(32)
    a = np.empty((k // 512, 16))
    for p in range(k // 512):
        a[p, :8] = np.random.permutation(np.resize(levels, 8))
        for g in range(8):
            far = levels[np.abs(levels - a[p, g]) >= 10]
            a[p, g + 8] = far[np.random.randint(len(far))]
    return np.exp2(a.ravel()).repeat(32)


BF16 = ml_dtypes.bfloat16


def bf(x):
    return np.asarray(x, np.float32).astype(BF16)


def f64(x):
    return np.asarray(x).astype(np.float64)


L, B, D, D0 = 512, 4, 1024, 768
EPS_BN = 1e-5
EPS_LN = 1e-5


def setup_inputs():
    n = np.random.standard_normal
    s = mx_kscale(D)
    r = n((B, L, D))
    return {"x": bf(n((L, B, D))), "res_a": bf(np.where(r > 0, r, 0.25 * r)),
            "ctx_v": bf(n((B, L, D)) * 0.25 * s), "W_v": bf(n((D, D)) * 2.0 / np.sqrt(D) / s[None, :]),
            "bn_v_g": bf(1.0 + 0.1 * n(D)), "bn_v_b": bf(0.2 * n(D)),
            "prelu_v": bf(0.25 + 0.05 * n(1)), "ln_g": bf(1.0 + 0.1 * n(D)), "ln_b": bf(0.2 * n(D))}


def core(x, res_a, ctx_v, W_v, bn_v_g, bn_v_b, prelu_v, ln_g, ln_b):
    xq = np.swapaxes(f64(x), 0, 1)
    y = mxq(f64(ctx_v), 2, "e4m3") @ mxq(f64(W_v), 1, "e4m3").T
    mean = y.mean(axis=(0, 1))
    var = y.var(axis=(0, 1))
    z = (y - mean) / np.sqrt(var + EPS_BN) * f64(bn_v_g) + f64(bn_v_b)
    res_v = np.where(z > 0, z, f64(prelu_v) * z)
    out = np.swapaxes(xq + f64(res_a) + res_v, 0, 1)
    mu = out.mean(axis=-1, keepdims=True)
    v = out.var(axis=-1, keepdims=True)
    return (out - mu) / np.sqrt(v + EPS_LN) * f64(ln_g) + f64(ln_b)


def e4m3fn_bytes(y):
    return np.clip(np.asarray(y, np.float64), -448.0, 448.0).astype(np.float32).astype(ml_dtypes.float8_e4m3fn).view(np.uint8)


def reference(x, res_a, ctx_v, W_v, bn_v_g, bn_v_b, prelu_v, ln_g, ln_b):
    out = core(x, res_a, ctx_v, W_v, bn_v_g, bn_v_b, prelu_v, ln_g, ln_b)
    s = np.max(np.abs(out)) / 448.0
    return out, e4m3fn_bytes(out / s)

@@ -1,0 +1,310 @@
+from contextlib import ExitStack
+
+import concourse.mybir as mybir
+from concourse.masks import make_identity
+
+L, B, D = 512, 4, 1024
+P = 128
+NC = D // P
+NQ = L // P
+EPS = 1e-5
+FLOPS = 2 * B * L * D * D
+
+F32 = mybir.dt.float32
+BF16 = mybir.dt.bfloat16
+U32 = mybir.dt.uint32
+U8 = mybir.dt.uint8
+FP8X4 = mybir.dt.float8_e4m3fn_x4
+FP8 = mybir.dt.float8_e4m3fn
+ALU = mybir.AluOpType
+ACT = mybir.ActivationFunctionType
+AX = mybir.AxisListType
+
+V_CAST = 2816
+
+
+def tile_coattention_pb_kernel(tc, x, res_a, ctx_v, W_v, bn_v_g, bn_v_b, prelu_v, ln_g, ln_b, out_0, out_1):
+    nc = tc.nc
+    ctx_rows = ctx_v.flatten_outer_dims()
+    out0_rows = out_0.rearrange("l b d -> l (b d)")
+    out1_rows = out_1.rearrange("l b d -> l (b d)")
+
+    with ExitStack() as es:
+        const = es.enter_context(tc.tile_pool(name="const", bufs=1))
+        small = es.enter_context(tc.tile_pool(name="small", bufs=4))
+        keep = es.enter_context(tc.tile_pool(name="keep", bufs=1))
+        xr = es.enter_context(tc.tile_pool(name="xr", bufs=1))
+        psum = es.enter_context(tc.psum_pool(name="psum", bufs=2))
+
+        eps_t = const.tile([P, 1], F32, name="eps_t")
+        nc.vector.memset(eps_t[:], EPS)
+        zero_t = const.tile([P, 1], F32, name="zero_t")
+        nc.vector.memset(zero_t[:], 0.0)
+        warm = const.tile([P, 1], F32, name="warm")
+        nc.scalar.activation(out=warm[:], in_=eps_t[:], func=ACT.Sqrt)
+        ident = const.tile([P, P], F32, name="ident")
+        make_identity(nc, ident[:])
+
+        pr_bf = const.tile([P, P], BF16, name="pr_bf")
+        nc.vector.memset(pr_bf[:], 0.0)
+        nc.sync.dma_start(out=pr_bf[0:NC, :], in_=bn_v_g.rearrange("(c p) -> c p", p=P))
+        nc.sync.dma_start(out=pr_bf[NC : 2 * NC, :], in_=bn_v_b.rearrange("(c p) -> c p", p=P))
+        p_bf = const.tile([P, 1], BF16, name="p_bf")
+        nc.sync.dma_start(out=p_bf[:], in_=prelu_v.partition_broadcast(P))
+
+        cc = keep.tile([P, 2, B * L], U32, name="cc", align_bytes=64)
+        cs = keep.tile([P, 2, B * L], U8, name="cs", align_bytes=64)
+        wc = keep.tile([P, 2, D], U32, name="wc", align_bytes=64)
+        ws = keep.tile([P, 2, D], U8, name="ws", align_bytes=64)
+        o_t = []
+        for lq in range(NQ):
+            o_lq = keep.tile([P, B, D], F32, name="o%d" % lq)
+            o_t.append(o_lq)
+
+        bank_no = [0]
+
+        def new_bank():
+            i = bank_no[0]
+            bank_no[0] = i + 1
+            if i % 4 == 3:
+                t_bank = psum.tile([P, 512], F32, name="tb", tag="t", bufs=2)
+                return t_bank
+            y_bank = psum.tile([P, 512], F32, name="yb", tag="y", bufs=6)
+            return y_bank
+
+        def evacuate(i, out, in_):
+            if i % 3 == 2:
+                nc.vector.tensor_copy(out=out, in_=in_)
+            else:
+                nc.scalar.copy(out=out, in_=in_)
+
+        with tc.tile_pool(name="stage", bufs=2) as stage:
+
+            def turn(rows_ap, dst_words, i):
+                raw = stage.tile([P, D], BF16, name="raw", tag="raw", bufs=8)
+                nc.sync.dma_start(out=raw[:], in_=rows_ap)
+                words = raw[:].bitcast(F32)
+                bank = new_bank()
+                for g in range(2):
+                    for u in range(2):
+                        j = 2 * g + u
+                        nc.tensor.transpose(bank[:, j * P : (j + 1) * P], words[:, 256 * g + u : 256 * (g + 1) : 2], ident[:])
+                evacuate(i, dst_words, bank[:].rearrange("p (g u r) -> p g r u", g=2, u=2))
+
+            def prep_w(c):
+                grw = stage.tile([P, 2, 4 * P], BF16, name="grw", tag="grw", bufs=2, align_bytes=64)
+                turn(W_v[c * P : (c + 1) * P, :], grw[:].bitcast(F32).rearrange("p g (r u) -> p g r u", u=2), c)
+                for g in range(2):
+                    nc.vector.quantize_mx(
+                        out=wc[:, g, c * P : (c + 1) * P].bitcast(FP8X4),
+                        scales=ws[:, g, c * P : (c + 1) * P],
+                        in_=grw[:, g, :],
+                    )
+
+            def prep_ctx(b):
+                gr = stage.tile([P, 2, 4 * L], BF16, name="gr", tag="gr", bufs=2, align_bytes=64)
+                grv = gr[:].bitcast(F32).rearrange("p g (r u) -> p g r u", u=2)
+                for lq in range(NQ):
+                    r0 = b * L + lq * P
+                    turn(ctx_rows[r0 : r0 + P, :], grv[:, :, lq * P : (lq + 1) * P, :], lq + 1)
+                for g in range(2):
+                    nc.vector.quantize_mx(
+                        out=cc[:, g, b * L : (b + 1) * L].bitcast(FP8X4),
+                        scales=cs[:, g, b * L : (b + 1) * L],
+                        in_=gr[:, g, :],
+                    )
+
+            pr_f = const.tile([P, P], F32, name="pr_f")
+            nc.vector.tensor_copy(out=pr_f[:], in_=pr_bf[:])
+            pt = new_bank()
+            nc.tensor.transpose(pt[:, 0:P], pr_f[:], ident[:])
+            prm = const.tile([P, 2 * NC], F32, name="prm")
+            nc.vector.tensor_copy(out=prm[:], in_=pt[:, 0 : 2 * NC])
+
+            for b in range(B):
+                prep_w(b)
+                prep_ctx(b)
+            for c in range(B, NC):
+                prep_w(c)
+
+        pf = const.tile([P, 1], F32, name="pf")
+        nc.vector.tensor_copy(out=pf[:], in_=p_bf[:])
+        sg = const.tile([P, 1], F32, name="sg")
+        nc.vector.tensor_scalar(out=sg[:], in0=pf[:], scalar1=1.0, scalar2=2.0, op0=ALU.is_le, op1=ALU.mult)
+        nc.vector.tensor_scalar(out=sg[:], in0=sg[:], scalar1=-1.0, scalar2=None, op0=ALU.add)
+        k4 = const.tile([P, 4], F32, name="k4")
+        nc.vector.tensor_tensor(out=k4[:, 0:1], in0=sg[:], in1=pf[:], op=ALU.mult)
+        nc.vector.tensor_tensor(out=k4[:, 1:2], in0=sg[:], in1=k4[:, 0:1], op=ALU.subtract)
+        nc.vector.tensor_scalar(out=k4[:, 2:4], in0=k4[:, 0:2], scalar1=-1.0, scalar2=None, op0=ALU.mult)
+        g4 = const.tile([P, NC, 4], F32, name="g4")
+        kb = const.tile([P, NC, 2], F32, name="kb")
+        for c in range(NC):
+            nc.gpsimd.tensor_scalar(out=g4[:, c, :], in0=k4[:], scalar1=prm[:, c : c + 1], scalar2=None, op0=ALU.mult)
+            nc.gpsimd.tensor_scalar(out=kb[:, c, :], in0=k4[:, 0:2], scalar1=prm[:, NC + c : NC + c + 1], scalar2=None, op0=ALU.mult)
+
+        xts = []
+        rts = []
+        for lq in range(NQ):
+            xt = xr.tile([P, B, D], BF16, name="xt%d" % lq)
+            nc.sync.dma_start(out=xt[:], in_=x[lq * P : (lq + 1) * P, :, :])
+            xts.append(xt)
+            rt = xr.tile([P, B, D], BF16, name="rt%d" % lq)
+            nc.sync.dma_start(out=rt[:], in_=res_a[:, lq * P : (lq + 1) * P, :].rearrange("b l d -> l b d"))
+            rts.append(rt)
+
+        def g_add(lq, c_lo, c_hi, first):
+            cols = slice(c_lo * P, c_hi * P)
+            src = xts[lq] if first else o_t[lq]
+            nc.gpsimd.tensor_tensor(out=o_t[lq][:, :, cols], in0=src[:, :, cols], in1=rts[lq][:, :, cols], op=ALU.add)
+
+        for lq in range(NQ):
+            mid = min(lq + 3, NC)
+            g_add(lq, lq + 1, mid, True)
+            if mid < NC:
+                g_add(lq, mid, NC, True)
+
+        g_bc = const.tile([P, D], BF16, name="g_bc")
+        nc.sync.dma_start(out=g_bc[:], in_=ln_g.partition_broadcast(P))
+        b_bc = const.tile([P, D], BF16, name="b_bc")
+        nc.sync.dma_start(out=b_bc[:], in_=ln_b.partition_broadcast(P))
+
+        with tc.tile_pool(name="q", bufs=3) as qp, tc.manual_schedule():
+            ys = {}
+            sts = {}
+            mvs = {}
+            sds = {}
+            prm_c = {}
+            qs = {}
+
+            def mm(c, b):
+                if b == 0:
+                    st = small.tile([P, B, 6], F32, name="st", tag="st")
+                    sts[c] = st
+                y = psum.tile([P, 512], F32, name="y", tag="y", bufs=6)
+                for g in range(2):
+                    nc.tensor.matmul_mx(
+                        out=y[:],
+                        lhsT=wc[:, g, c * P : (c + 1) * P].bitcast(FP8X4),
+                        lhsT_scale=ws[:, g, c * P : (c + 1) * P],
+                        rhs=cc[:, g, b * L : (b + 1) * L].bitcast(FP8X4),
+                        rhs_scale=cs[:, g, b * L : (b + 1) * L],
+                        start=(g == 0),
+                        stop=(g == 1),
+                    )
+                nc.vector.bn_stats(out=sts[c][:, b, :], in_=y[:])
+                ys[(c, b)] = y
+
+            def chain_a(c):
+                mv = small.tile([P, 2], F32, name="mv", tag="mv")
+                nc.vector.bn_aggr(out=mv[:], in_=sts[c][:].rearrange("p b s -> p (b s)"))
+                mvs[c] = mv
+
+            def chain_s(c):
+                sd = small.tile([P, 1], F32, name="sd", tag="sd")
+                nc.scalar.activation(out=sd[:], in_=mvs[c][:, 1:2], func=ACT.Sqrt, bias=eps_t[:, 0:1], scale=1.0)
+                sds[c] = sd
+
+            def chain_b(c):
+                rs = small.tile([P, 1], F32, name="rs", tag="rs")
+                nc.vector.reciprocal(out=rs[:], in_=sds[c][:])
+                sc4 = small.tile([P, 4], F32, name="sc4", tag="sc4")
+                nc.vector.tensor_scalar(out=sc4[:], in0=g4[:, c, :], scalar1=rs[:, 0:1], scalar2=None, op0=ALU.mult)
+                bi = small.tile([P, 2], F32, name="bi", tag="bi")
+                nc.vector.scalar_tensor_tensor(out=bi[:], in0=sc4[:, 2:4], scalar=mvs[c][:, 0:1], in1=kb[:, c, :], op0=ALU.mult, op1=ALU.add)
+                prm_c[c] = (sc4, bi)
+
+            def qq(c, b):
+                if b == 0:
+                    q1 = qp.tile([P, B * L], F32, name="q1", tag="q1")
+                    q2 = qp.tile([P, B * L], F32, name="q2", tag="q2")
+                    qs[c] = (q1, q2)
+                sc4, bi = prm_c[c]
+                y = ys[(c, b)]
+                nc.scalar.activation(out=qs[c][0][:, b * L : (b + 1) * L], in_=y[:], func=ACT.Identity, scale=sc4[:, 0:1], bias=bi[:, 0:1])
+                nc.scalar.activation(out=qs[c][1][:, b * L : (b + 1) * L], in_=y[:], func=ACT.Relu, scale=sc4[:, 1:2], bias=bi[:, 1:2])
+
+            def back(c, lq):
+                t = psum.tile([P, 512], F32, name="t", tag="t", bufs=2)
+                for b in range(B):
+                    col = b * L + lq * P
+                    nc.tensor.matmul(out=t[:, b * P : (b + 1) * P], lhsT=qs[c][0][:, col : col + P], rhs=ident[:], is_transpose=True, start=True, stop=False)
+                    nc.tensor.matmul(out=t[:, b * P : (b + 1) * P], lhsT=qs[c][1][:, col : col + P], rhs=ident[:], is_transpose=True, start=False, stop=True)
+                cols = slice(c * P, (c + 1) * P)
+                other = o_t[lq] if c > lq else xts[lq]
+                nc.vector.scalar_tensor_tensor(out=o_t[lq][:, :, cols], in0=t[:].rearrange("p (b n) -> p b n", b=B), scalar=sg[:, 0:1], in1=other[:, :, cols], op0=ALU.mult, op1=ALU.add)
+                if c == lq:
+                    g_add(lq, 0, lq + 1, False)
+
+            for b in range(B):
+                mm(0, b)
+            chain_a(0)
+            chain_s(0)
+            chain_b(0)
+            mm(1, 0)
+            mm(1, 1)
+            for c in range(NC + 1):
+                for b in range(B):
+                    if c < NC:
+                        qq(c, b)
+                    if b == 3 and c + 1 < NC:
+                        chain_s(c + 1)
+                    if c >= 1:
+                        back(c - 1, b)
+                    if b == 3 and c + 1 < NC:
+                        chain_b(c + 1)
+                    c2, b2 = divmod(4 * c + 6 + b, 4)
+                    if c2 < NC:
+                        mm(c2, b2)
+                    if b == 1 and c + 1 < NC:
+                        chain_a(c + 1)
+
+        with tc.tile_pool(name="tail", bufs=2) as tp:
+            am = const.tile([P, NQ * B], F32, name="am")
+            for lq in range(NQ):
+                nms = []
+                rss = []
+                for b in range(B):
+                    ov = o_t[lq][:, b, :]
+                    junk = tp.tile([P, D], BF16, name="junk", tag="junk")
+                    sm = small.tile([P, 1], F32, name="sm", tag="sm")
+                    nc.scalar.activation(out=junk[:], in_=ov, func=ACT.Copy, accum_out=sm[:])
+                    nm = small.tile([P, 1], F32, name="nm", tag="nm", bufs=8)
+                    nc.scalar.activation(out=nm[:], in_=sm[:], func=ACT.Copy, scale=-1.0 / D)
+                    junk2 = tp.tile([P, D], BF16, name="junk2", tag="junk")
+                    ss = small.tile([P, 1], F32, name="ss", tag="ss")
+                    nc.scalar.activation(out=junk2[:], in_=ov, func=ACT.Square, bias=nm[:, 0:1], scale=1.0, accum_out=ss[:])
+                    sd2 = small.tile([P, 1], F32, name="sd2", tag="sd2")
+                    nc.scalar.activation(out=sd2[:], in_=ss[:], func=ACT.Sqrt, bias=eps_t[:, 0:1], scale=1.0 / D)
+                    rs2 = small.tile([P, 1], F32, name="rs2", tag="rs2", bufs=8)
+                    nc.vector.reciprocal(out=rs2[:], in_=sd2[:])
+                    nms.append(nm)
+                    rss.append(rs2)
+                for b0 in range(0, B, 2):
+                    for b in (b0, b0 + 1):
+                        ov = o_t[lq][:, b, :]
+                        nc.vector.scalar_tensor_tensor(out=ov, in0=ov, scalar=nms[b][:, 0:1], in1=g_bc[:], op0=ALU.add, op1=ALU.mult)
+                    for b in (b0, b0 + 1):
+                        ov = o_t[lq][:, b, :]
+                        nc.vector.scalar_tensor_tensor(out=ov, in0=ov, scalar=rss[b][:, 0:1], in1=b_bc[:], op0=ALU.mult, op1=ALU.add)
+                    for b in (b0, b0 + 1):
+                        ov = o_t[lq][:, b, :]
+                        r = lq * B + b
+                        nc.vector.tensor_reduce(out=am[:, r : r + 1], in_=ov, axis=AX.X, op=ALU.max, apply_absolute_value=True)
+                        nc.sync.dma_start(out=out0_rows[lq * P : (lq + 1) * P, b * D : (b + 1) * D], in_=ov)
+
+            pm = small.tile([P, 1], F32, name="pm", tag="pm")
+            nc.vector.tensor_reduce(out=pm[:], in_=am[:], axis=AX.X, op=ALU.max)
+            tb2 = psum.tile([P, 512], F32, name="tb2", tag="t", bufs=2)
+            nc.tensor.transpose(tb2[:, 0:P], pm[:, 0:1].to_broadcast([P, P]), ident[:])
+            gm = small.tile([P, 1], F32, name="gm", tag="gm")
+            nc.vector.tensor_reduce(out=gm[:], in_=tb2[:, 0:P], axis=AX.X, op=ALU.max)
+            ri = small.tile([P, 1], F32, name="ri", tag="ri")
+            nc.vector.reciprocal(out=ri[:], in_=gm[:])
+            fac = small.tile([P, 1], F32, name="fac", tag="fac")
+            nc.vector.tensor_scalar(out=fac[:], in0=ri[:], scalar1=448.0, scalar2=None, op0=ALU.mult)
+            for lq in range(NQ):
+                of = o_t[lq][:].rearrange("p b d -> p (b d)")
+                f8 = tp.tile([P, B * D], FP8, name="f8", tag="f8", bufs=4)
+                nc.vector.tensor_scalar(out=f8[:, 0:V_CAST], in0=of[:, 0:V_CAST], scalar1=fac[:, 0:1], scalar2=None, op0=ALU.mult, saturate=False)
+                nc.scalar.activation(out=f8[:, V_CAST:], in_=of[:, V_CAST:], func=ACT.Identity, scale=fac[:, 0:1], bias=zero_t[:, 0:1], saturate=False)
+                nc.sync.dma_start(out=out1_rows[lq * P : (lq + 1) * P, :], in_=f8[:].bitcast(U8))

@@ -20,7 +20,8 @@ ALU = mybir.AluOpType
 ACT = mybir.ActivationFunctionType
 AX = mybir.AxisListType
 
-V_CAST = 2816
+V_CAST = 2752
+ORDER = (3, 0, 1, 2)
 
 
 def tile_coattention_pb_kernel(tc, x, res_a, ctx_v, W_v, bn_v_g, bn_v_b, prelu_v, ln_g, ln_b, out_0, out_1):
@@ -30,10 +31,11 @@ def tile_coattention_pb_kernel(tc, x, res_a, ctx_v, W_v, bn_v_g, bn_v_b, prelu_v
     out1_rows = out_1.rearrange("l b d -> l (b d)")
 
     with ExitStack() as es:
+        es.enter_context(tc.manual_schedule())
         const = es.enter_context(tc.tile_pool(name="const", bufs=1))
         small = es.enter_context(tc.tile_pool(name="small", bufs=4))
         keep = es.enter_context(tc.tile_pool(name="keep", bufs=1))
-        xr = es.enter_context(tc.tile_pool(name="xr", bufs=1))
+        xr = es.enter_context(tc.tile_pool(name="xr", bufs=4))
         psum = es.enter_context(tc.psum_pool(name="psum", bufs=2))
 
         eps_t = const.tile([P, 1], F32, name="eps_t")
@@ -41,7 +43,7 @@ def tile_coattention_pb_kernel(tc, x, res_a, ctx_v, W_v, bn_v_g, bn_v_b, prelu_v
         zero_t = const.tile([P, 1], F32, name="zero_t")
         nc.vector.memset(zero_t[:], 0.0)
         warm = const.tile([P, 1], F32, name="warm")
-        nc.scalar.activation(out=warm[:], in_=eps_t[:], func=ACT.Sqrt)
+        nc.scalar.activation(out=warm[:], in_=eps_t[:], func=ACT.Abs_reciprocal_sqrt)
         ident = const.tile([P, P], F32, name="ident")
         make_identity(nc, ident[:])
 
@@ -52,48 +54,80 @@ def tile_coattention_pb_kernel(tc, x, res_a, ctx_v, W_v, bn_v_g, bn_v_b, prelu_v
         p_bf = const.tile([P, 1], BF16, name="p_bf")
         nc.sync.dma_start(out=p_bf[:], in_=prelu_v.partition_broadcast(P))
 
-        cc = keep.tile([P, 2, B * L], U32, name="cc", align_bytes=64)
-        cs = keep.tile([P, 2, B * L], U8, name="cs", align_bytes=64)
-        wc = keep.tile([P, 2, D], U32, name="wc", align_bytes=64)
-        ws = keep.tile([P, 2, D], U8, name="ws", align_bytes=64)
         o_t = []
         for lq in range(NQ):
             o_lq = keep.tile([P, B, D], F32, name="o%d" % lq)
             o_t.append(o_lq)
+        ysb = []
+        for c in range(NC):
+            y_c = keep.tile([P, B * L], F32, name="ysb%d" % c)
+            ysb.append(y_c)
+        st = const.tile([P, NC, B, 6], F32, name="st")
+        sc4 = const.tile([P, NC, 4], F32, name="sc4")
+        bi = const.tile([P, NC, 2], F32, name="bi")
+        sums = const.tile([P, NQ * B, 2], F32, name="sums")
+        am = const.tile([P, NQ * B], F32, name="am")
+        g4 = const.tile([P, NC, 4], F32, name="g4")
+        kb = const.tile([P, NC, 2], F32, name="kb")
+        sg = const.tile([P, 1], F32, name="sg")
+        g_bc = const.tile([P, D], BF16, name="g_bc")
+        b_bc = const.tile([P, D], BF16, name="b_bc")
 
-        bank_no = [0]
+        q2s = {}
+        q2_first = keep.tile([P, NC, L], F32, name="q2_first")
+        q2s[ORDER[0]] = q2_first
 
-        def new_bank():
-            i = bank_no[0]
-            bank_no[0] = i + 1
-            if i % 4 == 3:
-                t_bank = psum.tile([P, 512], F32, name="tb", tag="t", bufs=2)
-                return t_bank
-            y_bank = psum.tile([P, 512], F32, name="yb", tag="y", bufs=6)
-            return y_bank
+        def parts(b, c, src):
+            nc.scalar.activation(out=q2s[b][:, c, :], in_=src, func=ACT.Relu, scale=sc4[:, c, 1:2], bias=bi[:, c, 1:2])
+            nc.scalar.activation(out=ysb[c][:, b * L : (b + 1) * L], in_=src, func=ACT.Identity, scale=sc4[:, c, 0:1], bias=bi[:, c, 0:1])
 
-        def evacuate(i, out, in_):
-            if i % 3 == 2:
-                nc.vector.tensor_copy(out=out, in_=in_)
-            else:
-                nc.scalar.copy(out=out, in_=in_)
+        def back(b, h, lq):
+            t = psum.tile([P, 512], F32, name="t", tag="y", bufs=5)
+            for j in range(4):
+                c = 4 * h + j
+                nc.tensor.matmul(out=t[:, j * P : (j + 1) * P], lhsT=ysb[c][:, b * L + lq * P : b * L + (lq + 1) * P], rhs=ident[:], is_transpose=True, start=True, stop=False)
+                nc.tensor.matmul(out=t[:, j * P : (j + 1) * P], lhsT=q2s[b][:, c, lq * P : (lq + 1) * P], rhs=ident[:], is_transpose=True, start=False, stop=True)
+            ov = o_t[lq][:, b, h * 512 : (h + 1) * 512]
+            r = b * NQ + lq
+            nc.vector.scalar_tensor_tensor(out=ov, in0=t[:], scalar=sg[:, 0:1], in1=ov, op0=ALU.mult, op1=ALU.add, accum_out=sums[:, r, h : h + 1])
 
-        with tc.tile_pool(name="stage", bufs=2) as stage:
+        def add_streams(b):
+            for lq in range(NQ):
+                xt = xr.tile([P, D], BF16, name="xt", tag="xt")
+                nc.sync.dma_start(out=xt[:], in_=x[lq * P : (lq + 1) * P, b, :])
+                rt = xr.tile([P, D], BF16, name="rt", tag="rt")
+                nc.sync.dma_start(out=rt[:], in_=res_a[b, lq * P : (lq + 1) * P, :])
+                nc.gpsimd.tensor_tensor(out=o_t[lq][:, b, :], in0=xt[:], in1=rt[:], op=ALU.add)
 
-            def turn(rows_ap, dst_words, i):
-                raw = stage.tile([P, D], BF16, name="raw", tag="raw", bufs=8)
+        with tc.tile_pool(name="codes", bufs=1) as codes, tc.tile_pool(name="stage", bufs=2) as stage:
+            cc = codes.tile([P, 2, B * L], U32, name="cc", align_bytes=64)
+            cs = codes.tile([P, 2, B * L], U8, name="cs", align_bytes=64)
+            wc = codes.tile([P, 2, D], U32, name="wc", align_bytes=64)
+            ws = codes.tile([P, 2, D], U8, name="ws", align_bytes=64)
+
+            raws = {}
+
+            def load(key, rows_ap):
+                raw = stage.tile([P, D], BF16, name="raw", tag="raw", bufs=6)
                 nc.sync.dma_start(out=raw[:], in_=rows_ap)
-                words = raw[:].bitcast(F32)
-                bank = new_bank()
+                raws[key] = raw
+
+            def turn(key, dst_words, on_vector):
+                words = raws[key][:].bitcast(F32)
+                bank = psum.tile([P, 512], F32, name="tb", tag="t", bufs=3)
                 for g in range(2):
                     for u in range(2):
                         j = 2 * g + u
                         nc.tensor.transpose(bank[:, j * P : (j + 1) * P], words[:, 256 * g + u : 256 * (g + 1) : 2], ident[:])
-                evacuate(i, dst_words, bank[:].rearrange("p (g u r) -> p g r u", g=2, u=2))
+                src = bank[:].rearrange("p (g u r) -> p g r u", g=2, u=2)
+                if on_vector:
+                    nc.vector.tensor_copy(out=dst_words, in_=src)
+                else:
+                    nc.scalar.copy(out=dst_words, in_=src)
 
             def prep_w(c):
                 grw = stage.tile([P, 2, 4 * P], BF16, name="grw", tag="grw", bufs=2, align_bytes=64)
-                turn(W_v[c * P : (c + 1) * P, :], grw[:].bitcast(F32).rearrange("p g (r u) -> p g r u", u=2), c)
+                turn(("w", c), grw[:].bitcast(F32).rearrange("p g (r u) -> p g r u", u=2), c % 2 == 1)
                 for g in range(2):
                     nc.vector.quantize_mx(
                         out=wc[:, g, c * P : (c + 1) * P].bitcast(FP8X4),
@@ -101,86 +135,25 @@ def tile_coattention_pb_kernel(tc, x, res_a, ctx_v, W_v, bn_v_g, bn_v_b, prelu_v
                         in_=grw[:, g, :],
                     )
 
-            def prep_ctx(b):
+            grs = {}
+
+            def turn_ctx(b):
                 gr = stage.tile([P, 2, 4 * L], BF16, name="gr", tag="gr", bufs=2, align_bytes=64)
+                grs[b] = gr
                 grv = gr[:].bitcast(F32).rearrange("p g (r u) -> p g r u", u=2)
                 for lq in range(NQ):
-                    r0 = b * L + lq * P
-                    turn(ctx_rows[r0 : r0 + P, :], grv[:, :, lq * P : (lq + 1) * P, :], lq + 1)
+                    turn(("c", b, lq), grv[:, :, lq * P : (lq + 1) * P, :], False)
+
+            def quant_ctx(b):
                 for g in range(2):
                     nc.vector.quantize_mx(
                         out=cc[:, g, b * L : (b + 1) * L].bitcast(FP8X4),
                         scales=cs[:, g, b * L : (b + 1) * L],
-                        in_=gr[:, g, :],
+                        in_=grs[b][:, g, :],
                     )
 
-            pr_f = const.tile([P, P], F32, name="pr_f")
-            nc.vector.tensor_copy(out=pr_f[:], in_=pr_bf[:])
-            pt = new_bank()
-            nc.tensor.transpose(pt[:, 0:P], pr_f[:], ident[:])
-            prm = const.tile([P, 2 * NC], F32, name="prm")
-            nc.vector.tensor_copy(out=prm[:], in_=pt[:, 0 : 2 * NC])
-
-            for b in range(B):
-                prep_w(b)
-                prep_ctx(b)
-            for c in range(B, NC):
-                prep_w(c)
-
-        pf = const.tile([P, 1], F32, name="pf")
-        nc.vector.tensor_copy(out=pf[:], in_=p_bf[:])
-        sg = const.tile([P, 1], F32, name="sg")
-        nc.vector.tensor_scalar(out=sg[:], in0=pf[:], scalar1=1.0, scalar2=2.0, op0=ALU.is_le, op1=ALU.mult)
-        nc.vector.tensor_scalar(out=sg[:], in0=sg[:], scalar1=-1.0, scalar2=None, op0=ALU.add)
-        k4 = const.tile([P, 4], F32, name="k4")
-        nc.vector.tensor_tensor(out=k4[:, 0:1], in0=sg[:], in1=pf[:], op=ALU.mult)
-        nc.vector.tensor_tensor(out=k4[:, 1:2], in0=sg[:], in1=k4[:, 0:1], op=ALU.subtract)
-        nc.vector.tensor_scalar(out=k4[:, 2:4], in0=k4[:, 0:2], scalar1=-1.0, scalar2=None, op0=ALU.mult)
-        g4 = const.tile([P, NC, 4], F32, name="g4")
-        kb = const.tile([P, NC, 2], F32, name="kb")
-        for c in range(NC):
-            nc.gpsimd.tensor_scalar(out=g4[:, c, :], in0=k4[:], scalar1=prm[:, c : c + 1], scalar2=None, op0=ALU.mult)
-            nc.gpsimd.tensor_scalar(out=kb[:, c, :], in0=k4[:, 0:2], scalar1=prm[:, NC + c : NC + c + 1], scalar2=None, op0=ALU.mult)
-
-        xts = []
-        rts = []
-        for lq in range(NQ):
-            xt = xr.tile([P, B, D], BF16, name="xt%d" % lq)
-            nc.sync.dma_start(out=xt[:], in_=x[lq * P : (lq + 1) * P, :, :])
-            xts.append(xt)
-            rt = xr.tile([P, B, D], BF16, name="rt%d" % lq)
-            nc.sync.dma_start(out=rt[:], in_=res_a[:, lq * P : (lq + 1) * P, :].rearrange("b l d -> l b d"))
-            rts.append(rt)
-
-        def g_add(lq, c_lo, c_hi, first):
-            cols = slice(c_lo * P, c_hi * P)
-            src = xts[lq] if first else o_t[lq]
-            nc.gpsimd.tensor_tensor(out=o_t[lq][:, :, cols], in0=src[:, :, cols], in1=rts[lq][:, :, cols], op=ALU.add)
-
-        for lq in range(NQ):
-            mid = min(lq + 3, NC)
-            g_add(lq, lq + 1, mid, True)
-            if mid < NC:
-                g_add(lq, mid, NC, True)
-
-        g_bc = const.tile([P, D], BF16, name="g_bc")
-        nc.sync.dma_start(out=g_bc[:], in_=ln_g.partition_broadcast(P))
-        b_bc = const.tile([P, D], BF16, name="b_bc")
-        nc.sync.dma_start(out=b_bc[:], in_=ln_b.partition_broadcast(P))
-
-        with tc.tile_pool(name="q", bufs=3) as qp, tc.manual_schedule():
-            ys = {}
-            sts = {}
-            mvs = {}
-            sds = {}
-            prm_c = {}
-            qs = {}
-
-            def mm(c, b):
-                if b == 0:
-                    st = small.tile([P, B, 6], F32, name="st", tag="st")
-                    sts[c] = st
-                y = psum.tile([P, 512], F32, name="y", tag="y", bufs=6)
+            def mm_a(c, b):
+                y = psum.tile([P, 512], F32, name="y", tag="y", bufs=5)
                 for g in range(2):
                     nc.tensor.matmul_mx(
                         out=y[:],
@@ -191,110 +164,132 @@ def tile_coattention_pb_kernel(tc, x, res_a, ctx_v, W_v, bn_v_g, bn_v_b, prelu_v
                         start=(g == 0),
                         stop=(g == 1),
                     )
-                nc.vector.bn_stats(out=sts[c][:, b, :], in_=y[:])
-                ys[(c, b)] = y
+                nc.vector.bn_stats(out=st[:, c, b, :], in_=y[:])
+                if b < B - 1:
+                    nc.scalar.copy(out=ysb[c][:, b * L : (b + 1) * L], in_=y[:])
+                else:
+                    chain(c)
+                    parts(b, c, y[:])
 
-            def chain_a(c):
+            def chain(c):
                 mv = small.tile([P, 2], F32, name="mv", tag="mv")
-                nc.vector.bn_aggr(out=mv[:], in_=sts[c][:].rearrange("p b s -> p (b s)"))
-                mvs[c] = mv
-
-            def chain_s(c):
-                sd = small.tile([P, 1], F32, name="sd", tag="sd")
-                nc.scalar.activation(out=sd[:], in_=mvs[c][:, 1:2], func=ACT.Sqrt, bias=eps_t[:, 0:1], scale=1.0)
-                sds[c] = sd
-
-            def chain_b(c):
+                nc.vector.bn_aggr(out=mv[:], in_=st[:, c, :, :].rearrange("p b s -> p (b s)"))
                 rs = small.tile([P, 1], F32, name="rs", tag="rs")
-                nc.vector.reciprocal(out=rs[:], in_=sds[c][:])
-                sc4 = small.tile([P, 4], F32, name="sc4", tag="sc4")
-                nc.vector.tensor_scalar(out=sc4[:], in0=g4[:, c, :], scalar1=rs[:, 0:1], scalar2=None, op0=ALU.mult)
-                bi = small.tile([P, 2], F32, name="bi", tag="bi")
-                nc.vector.scalar_tensor_tensor(out=bi[:], in0=sc4[:, 2:4], scalar=mvs[c][:, 0:1], in1=kb[:, c, :], op0=ALU.mult, op1=ALU.add)
-                prm_c[c] = (sc4, bi)
+                nc.scalar.activation(out=rs[:], in_=mv[:, 1:2], func=ACT.Abs_reciprocal_sqrt, bias=eps_t[:, 0:1], scale=1.0)
+                nc.scalar.activation(out=sc4[:, c, :], in_=g4[:, c, :], func=ACT.Copy, scale=rs[:, 0:1])
+                for i in range(2):
+                    nc.scalar.activation(out=bi[:, c, i : i + 1], in_=sc4[:, c, 2 + i : 3 + i], func=ACT.Identity, scale=mv[:, 0:1], bias=kb[:, c, i : i + 1])
 
-            def qq(c, b):
-                if b == 0:
-                    q1 = qp.tile([P, B * L], F32, name="q1", tag="q1")
-                    q2 = qp.tile([P, B * L], F32, name="q2", tag="q2")
-                    qs[c] = (q1, q2)
-                sc4, bi = prm_c[c]
-                y = ys[(c, b)]
-                nc.scalar.activation(out=qs[c][0][:, b * L : (b + 1) * L], in_=y[:], func=ACT.Identity, scale=sc4[:, 0:1], bias=bi[:, 0:1])
-                nc.scalar.activation(out=qs[c][1][:, b * L : (b + 1) * L], in_=y[:], func=ACT.Relu, scale=sc4[:, 1:2], bias=bi[:, 1:2])
+            for c in range(NC):
+                load(("w", c), W_v[c * P : (c + 1) * P, :])
 
-            def back(c, lq):
-                t = psum.tile([P, 512], F32, name="t", tag="t", bufs=2)
-                for b in range(B):
-                    col = b * L + lq * P
-                    nc.tensor.matmul(out=t[:, b * P : (b + 1) * P], lhsT=qs[c][0][:, col : col + P], rhs=ident[:], is_transpose=True, start=True, stop=False)
-                    nc.tensor.matmul(out=t[:, b * P : (b + 1) * P], lhsT=qs[c][1][:, col : col + P], rhs=ident[:], is_transpose=True, start=False, stop=True)
-                cols = slice(c * P, (c + 1) * P)
-                other = o_t[lq] if c > lq else xts[lq]
-                nc.vector.scalar_tensor_tensor(out=o_t[lq][:, :, cols], in0=t[:].rearrange("p (b n) -> p b n", b=B), scalar=sg[:, 0:1], in1=other[:, :, cols], op0=ALU.mult, op1=ALU.add)
-                if c == lq:
-                    g_add(lq, 0, lq + 1, False)
+            pr_f = const.tile([P, P], F32, name="pr_f")
+            nc.vector.tensor_copy(out=pr_f[:], in_=pr_bf[:])
+            pt = psum.tile([P, 512], F32, name="pt", tag="t", bufs=3)
+            nc.tensor.transpose(pt[:, 0:P], pr_f[:], ident[:])
+            prm = const.tile([P, 2 * NC], F32, name="prm")
+            nc.vector.tensor_copy(out=prm[:], in_=pt[:, 0 : 2 * NC])
+            pf = const.tile([P, 1], F32, name="pf")
+            nc.vector.tensor_copy(out=pf[:], in_=p_bf[:])
+            nc.vector.tensor_scalar(out=sg[:], in0=pf[:], scalar1=1.0, scalar2=2.0, op0=ALU.is_le, op1=ALU.mult)
+            nc.vector.tensor_scalar(out=sg[:], in0=sg[:], scalar1=-1.0, scalar2=None, op0=ALU.add)
+            k4 = const.tile([P, 4], F32, name="k4")
+            nc.vector.tensor_tensor(out=k4[:, 0:1], in0=sg[:], in1=pf[:], op=ALU.mult)
+            nc.vector.tensor_tensor(out=k4[:, 1:2], in0=sg[:], in1=k4[:, 0:1], op=ALU.subtract)
+            nc.vector.tensor_scalar(out=k4[:, 2:4], in0=k4[:, 0:2], scalar1=-1.0, scalar2=None, op0=ALU.mult)
+            for c in range(NC):
+                nc.gpsimd.tensor_scalar(out=g4[:, c, :], in0=k4[:], scalar1=prm[:, c : c + 1], scalar2=None, op0=ALU.mult)
+                nc.gpsimd.tensor_scalar(out=kb[:, c, :], in0=k4[:, 0:2], scalar1=prm[:, NC + c : NC + c + 1], scalar2=None, op0=ALU.mult)
 
+            for c in range(NC):
+                if c < NQ:
+                    load(("c", 0, c), ctx_rows[c * P : (c + 1) * P, :])
+                prep_w(c)
+            for lq in range(NQ):
+                load(("c", 1, lq), ctx_rows[L + lq * P : L + (lq + 1) * P, :])
+            turn_ctx(0)
+            quant_ctx(0)
             for b in range(B):
-                mm(0, b)
-            chain_a(0)
-            chain_s(0)
-            chain_b(0)
-            mm(1, 0)
-            mm(1, 1)
-            for c in range(NC + 1):
-                for b in range(B):
-                    if c < NC:
-                        qq(c, b)
-                    if b == 3 and c + 1 < NC:
-                        chain_s(c + 1)
-                    if c >= 1:
-                        back(c - 1, b)
-                    if b == 3 and c + 1 < NC:
-                        chain_b(c + 1)
-                    c2, b2 = divmod(4 * c + 6 + b, 4)
-                    if c2 < NC:
-                        mm(c2, b2)
-                    if b == 1 and c + 1 < NC:
-                        chain_a(c + 1)
+                if b + 2 < B:
+                    for lq in range(NQ):
+                        r0 = (b + 2) * L + lq * P
+                        load(("c", b + 2, lq), ctx_rows[r0 : r0 + P, :])
+                if b + 1 < B:
+                    turn_ctx(b + 1)
+                for c in range(NC):
+                    mm_a(c, b)
+                    if c == 3 and b + 1 < B:
+                        quant_ctx(b + 1)
+                    if b == B - 1 and c >= 4:
+                        back(b, 0, c - 4)
+                if b == 1:
+                    add_streams(ORDER[0])
+                    nc.sync.dma_start(out=g_bc[:], in_=ln_g.partition_broadcast(P))
+                    nc.sync.dma_start(out=b_bc[:], in_=ln_b.partition_broadcast(P))
+
+        for b in ORDER[1:]:
+            add_streams(b)
+
+        with tc.tile_pool(name="q", bufs=2) as qp:
+            nms = {}
+            rss = {}
+
+            def s_parts(b, h):
+                if h == 0:
+                    q2 = qp.tile([P, NC, L], F32, name="q2", tag="q2")
+                    q2s[b] = q2
+                for c in range(4 * h, 4 * h + 4):
+                    parts(b, c, ysb[c][:, b * L : (b + 1) * L])
+
+            def ln_stats(b, lq):
+                r = b * NQ + lq
+                ov = o_t[lq][:, b, :]
+                j2 = small.tile([P, 2], F32, name="j2", tag="j2")
+                nm = small.tile([P, 1], F32, name="nm", tag="nm", bufs=8)
+                nc.scalar.activation(out=j2[:], in_=sums[:, r, :], func=ACT.Copy, scale=-1.0 / D, accum_out=nm[:])
+                junk = qp.tile([P, D], BF16, name="junk", tag="junk")
+                ss = small.tile([P, 1], F32, name="ss", tag="ss")
+                nc.scalar.activation(out=junk[:], in_=ov, func=ACT.Square, bias=nm[:, 0:1], scale=1.0, accum_out=ss[:])
+                rs2 = small.tile([P, 1], F32, name="rs2", tag="rs2", bufs=8)
+                nc.scalar.activation(out=rs2[:], in_=ss[:], func=ACT.Abs_reciprocal_sqrt, bias=eps_t[:, 0:1], scale=1.0 / D)
+                nms[r] = nm
+                rss[r] = rs2
+
+            def ln_apply(b, lqs):
+                for lq in lqs:
+                    ov = o_t[lq][:, b, :]
+                    nc.vector.scalar_tensor_tensor(out=ov, in0=ov, scalar=nms[b * NQ + lq][:, 0:1], in1=g_bc[:], op0=ALU.add, op1=ALU.mult)
+                for lq in lqs:
+                    ov = o_t[lq][:, b, :]
+                    nc.vector.scalar_tensor_tensor(out=ov, in0=ov, scalar=rss[b * NQ + lq][:, 0:1], in1=b_bc[:], op0=ALU.mult, op1=ALU.add)
+                for lq in lqs:
+                    ov = o_t[lq][:, b, :]
+                    r = b * NQ + lq
+                    nc.vector.tensor_reduce(out=am[:, r : r + 1], in_=ov, axis=AX.X, op=ALU.max, apply_absolute_value=True)
+                    nc.sync.dma_start(out=out0_rows[lq * P : (lq + 1) * P, b * D : (b + 1) * D], in_=ov)
+
+            units = [(b, h) for b in ORDER for h in range(2)]
+            NU = len(units)
+            for n in range(2, NU + 2):
+                if n - 1 < NU:
+                    for lq in range(NQ):
+                        back(units[n - 1][0], units[n - 1][1], lq)
+                if n > 2 and n < NU:
+                    s_parts(units[n][0], units[n][1])
+                if n % 2 == 0:
+                    for lq in range(NQ):
+                        ln_stats(units[n - 2][0], lq)
+                if n == 2:
+                    s_parts(units[n][0], units[n][1])
+                if n % 2 == 0:
+                    ln_apply(units[n - 2][0], (0, 1))
+                else:
+                    ln_apply(units[n - 3][0], (2, 3))
 
         with tc.tile_pool(name="tail", bufs=2) as tp:
-            am = const.tile([P, NQ * B], F32, name="am")
-            for lq in range(NQ):
-                nms = []
-                rss = []
-                for b in range(B):
-                    ov = o_t[lq][:, b, :]
-                    junk = tp.tile([P, D], BF16, name="junk", tag="junk")
-                    sm = small.tile([P, 1], F32, name="sm", tag="sm")
-                    nc.scalar.activation(out=junk[:], in_=ov, func=ACT.Copy, accum_out=sm[:])
-                    nm = small.tile([P, 1], F32, name="nm", tag="nm", bufs=8)
-                    nc.scalar.activation(out=nm[:], in_=sm[:], func=ACT.Copy, scale=-1.0 / D)
-                    junk2 = tp.tile([P, D], BF16, name="junk2", tag="junk")
-                    ss = small.tile([P, 1], F32, name="ss", tag="ss")
-                    nc.scalar.activation(out=junk2[:], in_=ov, func=ACT.Square, bias=nm[:, 0:1], scale=1.0, accum_out=ss[:])
-                    sd2 = small.tile([P, 1], F32, name="sd2", tag="sd2")
-                    nc.scalar.activation(out=sd2[:], in_=ss[:], func=ACT.Sqrt, bias=eps_t[:, 0:1], scale=1.0 / D)
-                    rs2 = small.tile([P, 1], F32, name="rs2", tag="rs2", bufs=8)
-                    nc.vector.reciprocal(out=rs2[:], in_=sd2[:])
-                    nms.append(nm)
-                    rss.append(rs2)
-                for b0 in range(0, B, 2):
-                    for b in (b0, b0 + 1):
-                        ov = o_t[lq][:, b, :]
-                        nc.vector.scalar_tensor_tensor(out=ov, in0=ov, scalar=nms[b][:, 0:1], in1=g_bc[:], op0=ALU.add, op1=ALU.mult)
-                    for b in (b0, b0 + 1):
-                        ov = o_t[lq][:, b, :]
-                        nc.vector.scalar_tensor_tensor(out=ov, in0=ov, scalar=rss[b][:, 0:1], in1=b_bc[:], op0=ALU.mult, op1=ALU.add)
-                    for b in (b0, b0 + 1):
-                        ov = o_t[lq][:, b, :]
-                        r = lq * B + b
-                        nc.vector.tensor_reduce(out=am[:, r : r + 1], in_=ov, axis=AX.X, op=ALU.max, apply_absolute_value=True)
-                        nc.sync.dma_start(out=out0_rows[lq * P : (lq + 1) * P, b * D : (b + 1) * D], in_=ov)
-
             pm = small.tile([P, 1], F32, name="pm", tag="pm")
             nc.vector.tensor_reduce(out=pm[:], in_=am[:], axis=AX.X, op=ALU.max)
-            tb2 = psum.tile([P, 512], F32, name="tb2", tag="t", bufs=2)
+            tb2 = psum.tile([P, 512], F32, name="tb2", tag="t", bufs=3)
             nc.tensor.transpose(tb2[:, 0:P], pm[:, 0:1].to_broadcast([P, P]), ident[:])
             gm = small.tile([P, 1], F32, name="gm", tag="gm")
             nc.vector.tensor_reduce(out=gm[:], in_=tb2[:, 0:P], axis=AX.X, op=ALU.max)

@@ -22,6 +22,10 @@ AX = mybir.AxisListType
 
 V_CAST = 2752
 ORDER = (3, 0, 1, 2)
+PE_ADD = ((0, 0), (0, 1), (1, 0), (1, 1), (2, 0), (2, 1))
+AHEAD = 2
+V_EVERY = 0
+RAMP = 2
 
 
 def tile_coattention_pb_kernel(tc, x, res_a, ctx_v, W_v, bn_v_g, bn_v_b, prelu_v, ln_g, ln_b, out_0, out_1):
@@ -31,11 +35,11 @@ def tile_coattention_pb_kernel(tc, x, res_a, ctx_v, W_v, bn_v_g, bn_v_b, prelu_v
     out1_rows = out_1.rearrange("l b d -> l (b d)")
 
     with ExitStack() as es:
-        es.enter_context(tc.manual_schedule())
         const = es.enter_context(tc.tile_pool(name="const", bufs=1))
         small = es.enter_context(tc.tile_pool(name="small", bufs=4))
         keep = es.enter_context(tc.tile_pool(name="keep", bufs=1))
         xr = es.enter_context(tc.tile_pool(name="xr", bufs=4))
+        qp = es.enter_context(tc.tile_pool(name="q", bufs=2))
         psum = es.enter_context(tc.psum_pool(name="psum", bufs=2))
 
         eps_t = const.tile([P, 1], F32, name="eps_t")
@@ -58,10 +62,10 @@ def tile_coattention_pb_kernel(tc, x, res_a, ctx_v, W_v, bn_v_g, bn_v_b, prelu_v
         for lq in range(NQ):
             o_lq = keep.tile([P, B, D], F32, name="o%d" % lq)
             o_t.append(o_lq)
-        ysb = []
-        for c in range(NC):
-            y_c = keep.tile([P, B * L], F32, name="ysb%d" % c)
-            ysb.append(y_c)
+        cc = keep.tile([P, 2, B * L], U32, name="cc", align_bytes=64)
+        cs = keep.tile([P, 2, B * L], U8, name="cs", align_bytes=64)
+        wc = keep.tile([P, 2, D], U32, name="wc", align_bytes=64)
+        ws = keep.tile([P, 2, D], U8, name="ws", align_bytes=64)
         st = const.tile([P, NC, B, 6], F32, name="st")
         sc4 = const.tile([P, NC, 4], F32, name="sc4")
         bi = const.tile([P, NC, 2], F32, name="bi")
@@ -70,49 +74,84 @@ def tile_coattention_pb_kernel(tc, x, res_a, ctx_v, W_v, bn_v_g, bn_v_b, prelu_v
         g4 = const.tile([P, NC, 4], F32, name="g4")
         kb = const.tile([P, NC, 2], F32, name="kb")
         sg = const.tile([P, 1], F32, name="sg")
+        si_bf = const.tile([P, P], BF16, name="si_bf")
         g_bc = const.tile([P, D], BF16, name="g_bc")
         b_bc = const.tile([P, D], BF16, name="b_bc")
 
+        q1s = {}
         q2s = {}
-        q2_first = keep.tile([P, NC, L], F32, name="q2_first")
-        q2s[ORDER[0]] = q2_first
+        streams = {}
+        nms = {}
+        rss = {}
 
-        def parts(b, c, src):
-            nc.scalar.activation(out=q2s[b][:, c, :], in_=src, func=ACT.Relu, scale=sc4[:, c, 1:2], bias=bi[:, c, 1:2])
-            nc.scalar.activation(out=ysb[c][:, b * L : (b + 1) * L], in_=src, func=ACT.Identity, scale=sc4[:, c, 0:1], bias=bi[:, c, 0:1])
+        def mm(c, b, tag, bufs):
+            y = psum.tile([P, 512], F32, name="y", tag=tag, bufs=bufs)
+            for g in range(2):
+                nc.tensor.matmul_mx(
+                    out=y[:],
+                    lhsT=wc[:, g, c * P : (c + 1) * P].bitcast(FP8X4),
+                    lhsT_scale=ws[:, g, c * P : (c + 1) * P],
+                    rhs=cc[:, g, b * L : (b + 1) * L].bitcast(FP8X4),
+                    rhs_scale=cs[:, g, b * L : (b + 1) * L],
+                    start=(g == 0),
+                    stop=(g == 1),
+                )
+            return y
+
+        def parts(b, c, y):
+            if c == 0:
+                q1 = qp.tile([P, NC, L], F32, name="q1", tag="q1")
+                q2 = qp.tile([P, NC, L], F32, name="q2", tag="q2")
+                q1s[b] = q1
+                q2s[b] = q2
+            nc.scalar.activation(out=q2s[b][:, c, :], in_=y[:], func=ACT.Relu, scale=sc4[:, c, 1:2], bias=bi[:, c, 1:2])
+            nc.scalar.activation(out=q1s[b][:, c, :], in_=y[:], func=ACT.Identity, scale=sc4[:, c, 0:1], bias=bi[:, c, 0:1])
 
         def back(b, h, lq):
             t = psum.tile([P, 512], F32, name="t", tag="y", bufs=5)
+            on_pe = (b, lq) in PE_ADD
+            if on_pe:
+                for i in range(2):
+                    nc.tensor.matmul(out=t[:], lhsT=si_bf[:], rhs=streams[(b, lq)][i][:, h * 512 : (h + 1) * 512], start=(i == 0), stop=False)
             for j in range(4):
                 c = 4 * h + j
-                nc.tensor.matmul(out=t[:, j * P : (j + 1) * P], lhsT=ysb[c][:, b * L + lq * P : b * L + (lq + 1) * P], rhs=ident[:], is_transpose=True, start=True, stop=False)
-                nc.tensor.matmul(out=t[:, j * P : (j + 1) * P], lhsT=q2s[b][:, c, lq * P : (lq + 1) * P], rhs=ident[:], is_transpose=True, start=False, stop=True)
+                nc.tensor.matmul(out=t[:, j * P : (j + 1) * P], lhsT=q1s[b][:, c, lq * P : (lq + 1) * P], rhs=ident[:], is_transpose=True, start=not on_pe, stop=False)
+                nc.tensor.matmul(out=t[:, j * P : (j + 1) * P], lhsT=q2s[b][:, c, lq * P : (lq + 1) * P], rhs=ident[:], is_transpose=True, start=False, stop=(j == 3 or not on_pe))
             ov = o_t[lq][:, b, h * 512 : (h + 1) * 512]
             r = b * NQ + lq
-            nc.vector.scalar_tensor_tensor(out=ov, in0=t[:], scalar=sg[:, 0:1], in1=ov, op0=ALU.mult, op1=ALU.add, accum_out=sums[:, r, h : h + 1])
+            if on_pe:
+                nc.scalar.activation(out=ov, in_=t[:], func=ACT.Copy, scale=sg[:, 0:1], accum_out=sums[:, r, h : h + 1])
+            else:
+                nc.vector.scalar_tensor_tensor(out=ov, in0=t[:], scalar=sg[:, 0:1], in1=ov, op0=ALU.mult, op1=ALU.add, accum_out=sums[:, r, h : h + 1])
 
         def add_streams(b):
             for lq in range(NQ):
+                if (b, lq) in PE_ADD:
+                    continue
                 xt = xr.tile([P, D], BF16, name="xt", tag="xt")
                 nc.sync.dma_start(out=xt[:], in_=x[lq * P : (lq + 1) * P, b, :])
                 rt = xr.tile([P, D], BF16, name="rt", tag="rt")
                 nc.sync.dma_start(out=rt[:], in_=res_a[b, lq * P : (lq + 1) * P, :])
                 nc.gpsimd.tensor_tensor(out=o_t[lq][:, b, :], in0=xt[:], in1=rt[:], op=ALU.add)
 
-        with tc.tile_pool(name="codes", bufs=1) as codes, tc.tile_pool(name="stage", bufs=2) as stage:
-            cc = codes.tile([P, 2, B * L], U32, name="cc", align_bytes=64)
-            cs = codes.tile([P, 2, B * L], U8, name="cs", align_bytes=64)
-            wc = codes.tile([P, 2, D], U32, name="wc", align_bytes=64)
-            ws = codes.tile([P, 2, D], U8, name="ws", align_bytes=64)
+        def chain(c):
+            mv = small.tile([P, 2], F32, name="mv", tag="mv")
+            nc.vector.bn_aggr(out=mv[:], in_=st[:, c, :, :].rearrange("p b s -> p (b s)"))
+            rs = small.tile([P, 1], F32, name="rs", tag="rs")
+            nc.scalar.activation(out=rs[:], in_=mv[:, 1:2], func=ACT.Abs_reciprocal_sqrt, bias=eps_t[:, 0:1], scale=1.0)
+            nc.scalar.activation(out=sc4[:, c, :], in_=g4[:, c, :], func=ACT.Copy, scale=rs[:, 0:1])
+            for i in range(2):
+                nc.scalar.activation(out=bi[:, c, i : i + 1], in_=sc4[:, c, 2 + i : 3 + i], func=ACT.Identity, scale=mv[:, 0:1], bias=kb[:, c, i : i + 1])
 
+        with tc.tile_pool(name="stage", bufs=2) as stage:
             raws = {}
 
-            def load(key, rows_ap):
-                raw = stage.tile([P, D], BF16, name="raw", tag="raw", bufs=6)
-                nc.sync.dma_start(out=raw[:], in_=rows_ap)
+            def load(key):
+                raw = stage.tile([P, D], BF16, name="raw", tag="raw", bufs=8)
+                nc.sync.dma_start(out=raw[:], in_=(W_v if key[0] == "w" else ctx_rows)[key[1] * P : (key[1] + 1) * P, :])
                 raws[key] = raw
 
-            def turn(key, dst_words, on_vector):
+            def turn(key, dst, on_vector):
                 words = raws[key][:].bitcast(F32)
                 bank = psum.tile([P, 512], F32, name="tb", tag="t", bufs=3)
                 for g in range(2):
@@ -121,67 +160,23 @@ def tile_coattention_pb_kernel(tc, x, res_a, ctx_v, W_v, bn_v_g, bn_v_b, prelu_v
                         nc.tensor.transpose(bank[:, j * P : (j + 1) * P], words[:, 256 * g + u : 256 * (g + 1) : 2], ident[:])
                 src = bank[:].rearrange("p (g u r) -> p g r u", g=2, u=2)
                 if on_vector:
-                    nc.vector.tensor_copy(out=dst_words, in_=src)
+                    nc.vector.tensor_copy(out=dst, in_=src)
                 else:
-                    nc.scalar.copy(out=dst_words, in_=src)
+                    nc.scalar.copy(out=dst, in_=src)
 
-            def prep_w(c):
-                grw = stage.tile([P, 2, 4 * P], BF16, name="grw", tag="grw", bufs=2, align_bytes=64)
-                turn(("w", c), grw[:].bitcast(F32).rearrange("p g (r u) -> p g r u", u=2), c % 2 == 1)
+            def quant(key, gr):
+                codes_t, scales_t = (wc, ws) if key[0] == "w" else (cc, cs)
+                col = key[1] * P
                 for g in range(2):
                     nc.vector.quantize_mx(
-                        out=wc[:, g, c * P : (c + 1) * P].bitcast(FP8X4),
-                        scales=ws[:, g, c * P : (c + 1) * P],
-                        in_=grw[:, g, :],
+                        out=codes_t[:, g, col : col + 4 * P].bitcast(FP8X4),
+                        scales=scales_t[:, g, col : col + 4 * P],
+                        in_=gr[:, g, :],
                     )
 
-            grs = {}
-
-            def turn_ctx(b):
-                gr = stage.tile([P, 2, 4 * L], BF16, name="gr", tag="gr", bufs=2, align_bytes=64)
-                grs[b] = gr
-                grv = gr[:].bitcast(F32).rearrange("p g (r u) -> p g r u", u=2)
-                for lq in range(NQ):
-                    turn(("c", b, lq), grv[:, :, lq * P : (lq + 1) * P, :], False)
-
-            def quant_ctx(b):
-                for g in range(2):
-                    nc.vector.quantize_mx(
-                        out=cc[:, g, b * L : (b + 1) * L].bitcast(FP8X4),
-                        scales=cs[:, g, b * L : (b + 1) * L],
-                        in_=grs[b][:, g, :],
-                    )
-
-            def mm_a(c, b):
-                y = psum.tile([P, 512], F32, name="y", tag="y", bufs=5)
-                for g in range(2):
-                    nc.tensor.matmul_mx(
-                        out=y[:],
-                        lhsT=wc[:, g, c * P : (c + 1) * P].bitcast(FP8X4),
-                        lhsT_scale=ws[:, g, c * P : (c + 1) * P],
-                        rhs=cc[:, g, b * L : (b + 1) * L].bitcast(FP8X4),
-                        rhs_scale=cs[:, g, b * L : (b + 1) * L],
-                        start=(g == 0),
-                        stop=(g == 1),
-                    )
-                nc.vector.bn_stats(out=st[:, c, b, :], in_=y[:])
-                if b < B - 1:
-                    nc.scalar.copy(out=ysb[c][:, b * L : (b + 1) * L], in_=y[:])
-                else:
-                    chain(c)
-                    parts(b, c, y[:])
-
-            def chain(c):
-                mv = small.tile([P, 2], F32, name="mv", tag="mv")
-                nc.vector.bn_aggr(out=mv[:], in_=st[:, c, :, :].rearrange("p b s -> p (b s)"))
-                rs = small.tile([P, 1], F32, name="rs", tag="rs")
-                nc.scalar.activation(out=rs[:], in_=mv[:, 1:2], func=ACT.Abs_reciprocal_sqrt, bias=eps_t[:, 0:1], scale=1.0)
-                nc.scalar.activation(out=sc4[:, c, :], in_=g4[:, c, :], func=ACT.Copy, scale=rs[:, 0:1])
-                for i in range(2):
-                    nc.scalar.activation(out=bi[:, c, i : i + 1], in_=sc4[:, c, 2 + i : 3 + i], func=ACT.Identity, scale=mv[:, 0:1], bias=kb[:, c, i : i + 1])
-
-            for c in range(NC):
-                load(("w", c), W_v[c * P : (c + 1) * P, :])
+            jobs = [("w", c) for c in range(NC)] + [("c", i) for i in range(B * NQ)]
+            for key in jobs[:8]:
+                load(key)
 
             pr_f = const.tile([P, P], F32, name="pr_f")
             nc.vector.tensor_copy(out=pr_f[:], in_=pr_bf[:])
@@ -193,6 +188,7 @@ def tile_coattention_pb_kernel(tc, x, res_a, ctx_v, W_v, bn_v_g, bn_v_b, prelu_v
             nc.vector.tensor_copy(out=pf[:], in_=p_bf[:])
             nc.vector.tensor_scalar(out=sg[:], in0=pf[:], scalar1=1.0, scalar2=2.0, op0=ALU.is_le, op1=ALU.mult)
             nc.vector.tensor_scalar(out=sg[:], in0=sg[:], scalar1=-1.0, scalar2=None, op0=ALU.add)
+            nc.vector.tensor_scalar(out=si_bf[:], in0=ident[:], scalar1=sg[:, 0:1], scalar2=None, op0=ALU.mult)
             k4 = const.tile([P, 4], F32, name="k4")
             nc.vector.tensor_tensor(out=k4[:, 0:1], in0=sg[:], in1=pf[:], op=ALU.mult)
             nc.vector.tensor_tensor(out=k4[:, 1:2], in0=sg[:], in1=k4[:, 0:1], op=ALU.subtract)
@@ -201,45 +197,48 @@ def tile_coattention_pb_kernel(tc, x, res_a, ctx_v, W_v, bn_v_g, bn_v_b, prelu_v
                 nc.gpsimd.tensor_scalar(out=g4[:, c, :], in0=k4[:], scalar1=prm[:, c : c + 1], scalar2=None, op0=ALU.mult)
                 nc.gpsimd.tensor_scalar(out=kb[:, c, :], in0=k4[:, 0:2], scalar1=prm[:, NC + c : NC + c + 1], scalar2=None, op0=ALU.mult)
 
-            for c in range(NC):
-                if c < NQ:
-                    load(("c", 0, c), ctx_rows[c * P : (c + 1) * P, :])
-                prep_w(c)
-            for lq in range(NQ):
-                load(("c", 1, lq), ctx_rows[L + lq * P : L + (lq + 1) * P, :])
-            turn_ctx(0)
-            quant_ctx(0)
-            for b in range(B):
-                if b + 2 < B:
-                    for lq in range(NQ):
-                        r0 = (b + 2) * L + lq * P
-                        load(("c", b + 2, lq), ctx_rows[r0 : r0 + P, :])
-                if b + 1 < B:
-                    turn_ctx(b + 1)
+            def do_group(i0):
+                gr = stage.tile([P, 2, 16 * P], BF16, name="gr", tag="gr", bufs=2, align_bytes=64)
+                grv = gr[:].bitcast(F32).rearrange("p g (r u) -> p g r u", u=2)
+                for i in range(i0, i0 + 4):
+                    if i + 8 < len(jobs):
+                        load(jobs[i + 8])
+                    turn(jobs[i], grv[:, :, (i - i0) * P : (i - i0 + 1) * P, :], V_EVERY > 0 and i % V_EVERY == V_EVERY - 1)
+                quant(jobs[i0], gr)
+
+            def stats_batch(b):
                 for c in range(NC):
-                    mm_a(c, b)
-                    if c == 3 and b + 1 < B:
-                        quant_ctx(b + 1)
-                    if b == B - 1 and c >= 4:
-                        back(b, 0, c - 4)
-                if b == 1:
-                    add_streams(ORDER[0])
-                    nc.sync.dma_start(out=g_bc[:], in_=ln_g.partition_broadcast(P))
-                    nc.sync.dma_start(out=b_bc[:], in_=ln_b.partition_broadcast(P))
+                    y = mm(c, b, "y", 5)
+                    nc.vector.bn_stats(out=st[:, c, b, :], in_=y[:])
+                    if b == B - 1:
+                        chain(c)
+                        parts(b, c, y)
+                        if c >= 4:
+                            back(b, 0, c - 4)
 
-        for b in ORDER[1:]:
-            add_streams(b)
+            def load_streams():
+                for b in ORDER:
+                    add_streams(b)
+                    if b == ORDER[0]:
+                        nc.sync.dma_start(out=g_bc[:], in_=ln_g.partition_broadcast(P))
+                        nc.sync.dma_start(out=b_bc[:], in_=ln_b.partition_broadcast(P))
 
-        with tc.tile_pool(name="q", bufs=2) as qp:
-            nms = {}
-            rss = {}
+            for i0 in range(0, NC + AHEAD * NQ, 4):
+                do_group(i0)
+            for b in range(B):
+                if b + AHEAD < B:
+                    do_group(NC + (b + AHEAD) * NQ)
+                if b == B - AHEAD:
+                    load_streams()
+                stats_batch(b)
 
-            def s_parts(b, h):
-                if h == 0:
-                    q2 = qp.tile([P, NC, L], F32, name="q2", tag="q2")
-                    q2s[b] = q2
-                for c in range(4 * h, 4 * h + 4):
-                    parts(b, c, ysb[c][:, b * L : (b + 1) * L])
+        with tc.tile_pool(name="late", bufs=2) as late:
+            for b, lq in PE_ADD:
+                xa = late.tile([P, D], BF16, name="xa%d%d" % (b, lq), bufs=1)
+                nc.sync.dma_start(out=xa[:], in_=x[lq * P : (lq + 1) * P, b, :])
+                ra = late.tile([P, D], BF16, name="ra%d%d" % (b, lq), bufs=1)
+                nc.sync.dma_start(out=ra[:], in_=res_a[b, lq * P : (lq + 1) * P, :])
+                streams[(b, lq)] = (xa, ra)
 
             def ln_stats(b, lq):
                 r = b * NQ + lq
@@ -247,7 +246,7 @@ def tile_coattention_pb_kernel(tc, x, res_a, ctx_v, W_v, bn_v_g, bn_v_b, prelu_v
                 j2 = small.tile([P, 2], F32, name="j2", tag="j2")
                 nm = small.tile([P, 1], F32, name="nm", tag="nm", bufs=8)
                 nc.scalar.activation(out=j2[:], in_=sums[:, r, :], func=ACT.Copy, scale=-1.0 / D, accum_out=nm[:])
-                junk = qp.tile([P, D], BF16, name="junk", tag="junk")
+                junk = late.tile([P, D], BF16, name="junk", tag="junk")
                 ss = small.tile([P, 1], F32, name="ss", tag="ss")
                 nc.scalar.activation(out=junk[:], in_=ov, func=ACT.Square, bias=nm[:, 0:1], scale=1.0, accum_out=ss[:])
                 rs2 = small.tile([P, 1], F32, name="rs2", tag="rs2", bufs=8)
@@ -268,25 +267,30 @@ def tile_coattention_pb_kernel(tc, x, res_a, ctx_v, W_v, bn_v_g, bn_v_b, prelu_v
                     nc.vector.tensor_reduce(out=am[:, r : r + 1], in_=ov, axis=AX.X, op=ALU.max, apply_absolute_value=True)
                     nc.sync.dma_start(out=out0_rows[lq * P : (lq + 1) * P, b * D : (b + 1) * D], in_=ov)
 
+            def mm_parts(u, j):
+                c = 4 * u[1] + j
+                y = mm(c, u[0], "t", 3)
+                parts(u[0], c, y)
+
             units = [(b, h) for b in ORDER for h in range(2)]
             NU = len(units)
             for n in range(2, NU + 2):
-                if n - 1 < NU:
-                    for lq in range(NQ):
-                        back(units[n - 1][0], units[n - 1][1], lq)
-                if n > 2 and n < NU:
-                    s_parts(units[n][0], units[n][1])
+                first = RAMP if n == 2 else 4
+                for j in range(4):
+                    if n < NU and j < first:
+                        mm_parts(units[n], j)
+                    if n - 1 < NU:
+                        back(units[n - 1][0], units[n - 1][1], j)
                 if n % 2 == 0:
                     for lq in range(NQ):
                         ln_stats(units[n - 2][0], lq)
-                if n == 2:
-                    s_parts(units[n][0], units[n][1])
+                for j in range(first, 4):
+                    mm_parts(units[n], j)
                 if n % 2 == 0:
                     ln_apply(units[n - 2][0], (0, 1))
                 else:
                     ln_apply(units[n - 3][0], (2, 3))
 
-        with tc.tile_pool(name="tail", bufs=2) as tp:
             pm = small.tile([P, 1], F32, name="pm", tag="pm")
             nc.vector.tensor_reduce(out=pm[:], in_=am[:], axis=AX.X, op=ALU.max)
             tb2 = psum.tile([P, 512], F32, name="tb2", tag="t", bufs=3)
@@ -299,7 +303,7 @@ def tile_coattention_pb_kernel(tc, x, res_a, ctx_v, W_v, bn_v_g, bn_v_b, prelu_v
             nc.vector.tensor_scalar(out=fac[:], in0=ri[:], scalar1=448.0, scalar2=None, op0=ALU.mult)
             for lq in range(NQ):
                 of = o_t[lq][:].rearrange("p b d -> p (b d)")
-                f8 = tp.tile([P, B * D], FP8, name="f8", tag="f8", bufs=4)
+                f8 = late.tile([P, B * D], FP8, name="f8", tag="f8", bufs=4)
                 nc.vector.tensor_scalar(out=f8[:, 0:V_CAST], in0=of[:, 0:V_CAST], scalar1=fac[:, 0:1], scalar2=None, op0=ALU.mult, saturate=False)
                 nc.scalar.activation(out=f8[:, V_CAST:], in_=of[:, V_CAST:], func=ACT.Identity, scale=fac[:, 0:1], bias=zero_t[:, 0:1], saturate=False)
                 nc.sync.dma_start(out=out1_rows[lq * P : (lq + 1) * P, :], in_=f8[:].bitcast(U8))

@@ -23,7 +23,6 @@ AX = mybir.AxisListType
 V_CAST = 2752
 ORDER = (3, 0, 1, 2)
 PE_ADD = ((0, 0), (0, 1), (1, 0), (1, 1), (2, 0), (2, 1))
-AHEAD = 2
 V_EVERY = 0
 RAMP = 2
 
@@ -38,7 +37,6 @@ def tile_coattention_pb_kernel(tc, x, res_a, ctx_v, W_v, bn_v_g, bn_v_b, prelu_v
         const = es.enter_context(tc.tile_pool(name="const", bufs=1))
         small = es.enter_context(tc.tile_pool(name="small", bufs=4))
         keep = es.enter_context(tc.tile_pool(name="keep", bufs=1))
-        xr = es.enter_context(tc.tile_pool(name="xr", bufs=4))
         qp = es.enter_context(tc.tile_pool(name="q", bufs=2))
         psum = es.enter_context(tc.psum_pool(name="psum", bufs=2))
 
@@ -75,9 +73,8 @@ def tile_coattention_pb_kernel(tc, x, res_a, ctx_v, W_v, bn_v_g, bn_v_b, prelu_v
         kb = const.tile([P, NC, 2], F32, name="kb")
         sg = const.tile([P, 1], F32, name="sg")
         si_bf = const.tile([P, P], BF16, name="si_bf")
-        g_bc = const.tile([P, D], BF16, name="g_bc")
-        b_bc = const.tile([P, D], BF16, name="b_bc")
 
+        pools = {}
         q1s = {}
         q2s = {}
         streams = {}
@@ -128,9 +125,9 @@ def tile_coattention_pb_kernel(tc, x, res_a, ctx_v, W_v, bn_v_g, bn_v_b, prelu_v
             for lq in range(NQ):
                 if (b, lq) in PE_ADD:
                     continue
-                xt = xr.tile([P, D], BF16, name="xt", tag="xt")
+                xt = pools["late"].tile([P, D], BF16, name="xt", tag="xt", bufs=4)
                 nc.sync.dma_start(out=xt[:], in_=x[lq * P : (lq + 1) * P, b, :])
-                rt = xr.tile([P, D], BF16, name="rt", tag="rt")
+                rt = pools["late"].tile([P, D], BF16, name="rt", tag="rt", bufs=4)
                 nc.sync.dma_start(out=rt[:], in_=res_a[b, lq * P : (lq + 1) * P, :])
                 nc.gpsimd.tensor_tensor(out=o_t[lq][:, b, :], in0=xt[:], in1=rt[:], op=ALU.add)
 
@@ -206,39 +203,35 @@ def tile_coattention_pb_kernel(tc, x, res_a, ctx_v, W_v, bn_v_g, bn_v_b, prelu_v
                     turn(jobs[i], grv[:, :, (i - i0) * P : (i - i0 + 1) * P, :], V_EVERY > 0 and i % V_EVERY == V_EVERY - 1)
                 quant(jobs[i0], gr)
 
-            def stats_batch(b):
-                for c in range(NC):
-                    y = mm(c, b, "y", 5)
-                    nc.vector.bn_stats(out=st[:, c, b, :], in_=y[:])
-                    if b == B - 1:
-                        chain(c)
-                        parts(b, c, y)
-                        if c >= 4:
-                            back(b, 0, c - 4)
-
-            def load_streams():
-                for b in ORDER:
-                    add_streams(b)
-                    if b == ORDER[0]:
-                        nc.sync.dma_start(out=g_bc[:], in_=ln_g.partition_broadcast(P))
-                        nc.sync.dma_start(out=b_bc[:], in_=ln_b.partition_broadcast(P))
-
-            for i0 in range(0, NC + AHEAD * NQ, 4):
+            for i0 in range(0, len(jobs), 4):
                 do_group(i0)
-            for b in range(B):
-                if b + AHEAD < B:
-                    do_group(NC + (b + AHEAD) * NQ)
-                if b == B - AHEAD:
-                    load_streams()
-                stats_batch(b)
 
         with tc.tile_pool(name="late", bufs=2) as late:
+            pools["late"] = late
+            g_bc = late.tile([P, D], BF16, name="g_bc", bufs=1)
+            b_bc = late.tile([P, D], BF16, name="b_bc", bufs=1)
+            for b in ORDER:
+                add_streams(b)
+                if b == ORDER[0]:
+                    nc.sync.dma_start(out=g_bc[:], in_=ln_g.partition_broadcast(P))
+                    nc.sync.dma_start(out=b_bc[:], in_=ln_b.partition_broadcast(P))
             for b, lq in PE_ADD:
                 xa = late.tile([P, D], BF16, name="xa%d%d" % (b, lq), bufs=1)
                 nc.sync.dma_start(out=xa[:], in_=x[lq * P : (lq + 1) * P, b, :])
                 ra = late.tile([P, D], BF16, name="ra%d%d" % (b, lq), bufs=1)
                 nc.sync.dma_start(out=ra[:], in_=res_a[b, lq * P : (lq + 1) * P, :])
                 streams[(b, lq)] = (xa, ra)
+
+            for b in range(B):
+                for c in range(NC):
+                    y = mm(c, b, "y", 5)
+                    nc.vector.bn_stats(out=st[:, c, b, :], in_=y[:])
+                    if b == B - 1:
+                        with tc.high_priority():
+                            chain(c)
+                        parts(b, c, y)
+                        if c >= 4:
+                            back(b, 0, c - 4)
 
             def ln_stats(b, lq):
                 r = b * NQ + lq
@@ -282,8 +275,9 @@ def tile_coattention_pb_kernel(tc, x, res_a, ctx_v, W_v, bn_v_g, bn_v_b, prelu_v
                     if n - 1 < NU:
                         back(units[n - 1][0], units[n - 1][1], j)
                 if n % 2 == 0:
-                    for lq in range(NQ):
-                        ln_stats(units[n - 2][0], lq)
+                    with tc.high_priority():
+                        for lq in range(NQ):
+                            ln_stats(units[n - 2][0], lq)
                 for j in range(first, 4):
                     mm_parts(units[n], j)
                 if n % 2 == 0:
@@ -304,6 +298,11 @@ def tile_coattention_pb_kernel(tc, x, res_a, ctx_v, W_v, bn_v_g, bn_v_b, prelu_v
             for lq in range(NQ):
                 of = o_t[lq][:].rearrange("p b d -> p (b d)")
                 f8 = late.tile([P, B * D], FP8, name="f8", tag="f8", bufs=4)
-                nc.vector.tensor_scalar(out=f8[:, 0:V_CAST], in0=of[:, 0:V_CAST], scalar1=fac[:, 0:1], scalar2=None, op0=ALU.mult, saturate=False)
-                nc.scalar.activation(out=f8[:, V_CAST:], in_=of[:, V_CAST:], func=ACT.Identity, scale=fac[:, 0:1], bias=zero_t[:, 0:1], saturate=False)
-                nc.sync.dma_start(out=out1_rows[lq * P : (lq + 1) * P, :], in_=f8[:].bitcast(U8))
+                if lq < NQ - 1:
+                    cuts = ((0, V_CAST, B * D),)
+                else:
+                    cuts = ((0, V_CAST // 2, B * D // 2), (B * D // 2, B * D // 2 + V_CAST // 2, B * D))
+                for lo, mid, hi in cuts:
+                    nc.vector.tensor_scalar(out=f8[:, lo:mid], in0=of[:, lo:mid], scalar1=fac[:, 0:1], scalar2=None, op0=ALU.mult, saturate=False)
+                    nc.scalar.activation(out=f8[:, mid:hi], in_=of[:, mid:hi], func=ACT.Identity, scale=fac[:, 0:1], bias=zero_t[:, 0:1], saturate=False)
+                    nc.sync.dma_start(out=out1_rows[lq * P : (lq + 1) * P, lo:hi], in_=f8[:, lo:hi].bitcast(U8))

@@ -24,6 +24,8 @@ V_CAST = 2752
 ORDER = (3, 0, 1, 2)
 PE_ADD = ((0, 0), (0, 1), (1, 0), (1, 1), (2, 0), (2, 1))
 V_EVERY = 0
+V_Q1 = ()
+G_LQ = (1,)
 RAMP = 2
 
 
@@ -102,7 +104,10 @@ def tile_coattention_pb_kernel(tc, x, res_a, ctx_v, W_v, bn_v_g, bn_v_b, prelu_v
                 q1s[b] = q1
                 q2s[b] = q2
             nc.scalar.activation(out=q2s[b][:, c, :], in_=y[:], func=ACT.Relu, scale=sc4[:, c, 1:2], bias=bi[:, c, 1:2])
-            nc.scalar.activation(out=q1s[b][:, c, :], in_=y[:], func=ACT.Identity, scale=sc4[:, c, 0:1], bias=bi[:, c, 0:1])
+            if c in V_Q1:
+                nc.vector.tensor_scalar(out=q1s[b][:, c, :], in0=y[:], scalar1=sc4[:, c, 0:1], scalar2=bi[:, c, 0:1], op0=ALU.mult, op1=ALU.add)
+            else:
+                nc.scalar.activation(out=q1s[b][:, c, :], in_=y[:], func=ACT.Identity, scale=sc4[:, c, 0:1], bias=bi[:, c, 0:1])
 
         def back(b, h, lq):
             t = psum.tile([P, 512], F32, name="t", tag="y", bufs=5)
@@ -247,11 +252,21 @@ def tile_coattention_pb_kernel(tc, x, res_a, ctx_v, W_v, bn_v_g, bn_v_b, prelu_v
                 nms[r] = nm
                 rss[r] = rs2
 
+            def g_apply(b, lq):
+                ov = o_t[lq][:, b, :]
+                nc.gpsimd.tensor_scalar(out=ov, in0=ov, scalar1=nms[b * NQ + lq][:, 0:1], scalar2=rss[b * NQ + lq][:, 0:1], op0=ALU.add, op1=ALU.mult)
+                nc.gpsimd.tensor_tensor(out=ov, in0=ov, in1=g_bc[:], op=ALU.mult)
+                nc.gpsimd.tensor_tensor(out=ov, in0=ov, in1=b_bc[:], op=ALU.add)
+
             def ln_apply(b, lqs):
                 for lq in lqs:
+                    if lq in G_LQ:
+                        continue
                     ov = o_t[lq][:, b, :]
                     nc.vector.scalar_tensor_tensor(out=ov, in0=ov, scalar=nms[b * NQ + lq][:, 0:1], in1=g_bc[:], op0=ALU.add, op1=ALU.mult)
                 for lq in lqs:
+                    if lq in G_LQ:
+                        continue
                     ov = o_t[lq][:, b, :]
                     nc.vector.scalar_tensor_tensor(out=ov, in0=ov, scalar=rss[b * NQ + lq][:, 0:1], in1=b_bc[:], op0=ALU.mult, op1=ALU.add)
                 for lq in lqs:
@@ -276,8 +291,12 @@ def tile_coattention_pb_kernel(tc, x, res_a, ctx_v, W_v, bn_v_g, bn_v_b, prelu_v
                         back(units[n - 1][0], units[n - 1][1], j)
                 if n % 2 == 0:
                     with tc.high_priority():
-                        for lq in range(NQ):
+                        for lq in G_LQ:
                             ln_stats(units[n - 2][0], lq)
+                            g_apply(units[n - 2][0], lq)
+                        for lq in range(NQ):
+                            if lq not in G_LQ:
+                                ln_stats(units[n - 2][0], lq)
                 for j in range(first, 4):
                     mm_parts(units[n], j)
                 if n % 2 == 0:

@@ -24,6 +24,8 @@ V_CAST = 2752
 ORDER = (3, 0, 1, 2)
 PE_ADD = ((0, 0), (0, 1), (1, 0), (1, 1), (2, 0), (2, 1))
 V_EVERY = 0
+NT = 3
+NY = 3
 V_Q1 = ()
 G_LQ = (1,)
 RAMP = 2
@@ -55,6 +57,10 @@ def tile_coattention_pb_kernel(tc, x, res_a, ctx_v, W_v, bn_v_g, bn_v_b, prelu_v
         nc.vector.memset(pr_bf[:], 0.0)
         nc.sync.dma_start(out=pr_bf[0:NC, :], in_=bn_v_g.rearrange("(c p) -> c p", p=P))
         nc.sync.dma_start(out=pr_bf[NC : 2 * NC, :], in_=bn_v_b.rearrange("(c p) -> c p", p=P))
+        nc.sync.dma_start(out=pr_bf[2 * NC : 3 * NC, :], in_=ln_g.rearrange("(c p) -> c p", p=P))
+        nc.sync.dma_start(out=pr_bf[3 * NC : 4 * NC, :], in_=ln_b.rearrange("(c p) -> c p", p=P))
+        ident_bf = const.tile([P, P], BF16, name="ident_bf")
+        make_identity(nc, ident_bf[:])
         p_bf = const.tile([P, 1], BF16, name="p_bf")
         nc.sync.dma_start(out=p_bf[:], in_=prelu_v.partition_broadcast(P))
 
@@ -110,7 +116,7 @@ def tile_coattention_pb_kernel(tc, x, res_a, ctx_v, W_v, bn_v_g, bn_v_b, prelu_v
                 nc.scalar.activation(out=q1s[b][:, c, :], in_=y[:], func=ACT.Identity, scale=sc4[:, c, 0:1], bias=bi[:, c, 0:1])
 
         def back(b, h, lq):
-            t = psum.tile([P, 512], F32, name="t", tag="y", bufs=5)
+            t = psum.tile([P, 512], F32, name="t", tag="y", bufs=NY)
             on_pe = (b, lq) in PE_ADD
             if on_pe:
                 for i in range(2):
@@ -155,7 +161,7 @@ def tile_coattention_pb_kernel(tc, x, res_a, ctx_v, W_v, bn_v_g, bn_v_b, prelu_v
 
             def turn(key, dst, on_vector):
                 words = raws[key][:].bitcast(F32)
-                bank = psum.tile([P, 512], F32, name="tb", tag="t", bufs=3)
+                bank = psum.tile([P, 512], F32, name="tb", tag="t", bufs=NT)
                 for g in range(2):
                     for u in range(2):
                         j = 2 * g + u
@@ -182,10 +188,17 @@ def tile_coattention_pb_kernel(tc, x, res_a, ctx_v, W_v, bn_v_g, bn_v_b, prelu_v
 
             pr_f = const.tile([P, P], F32, name="pr_f")
             nc.vector.tensor_copy(out=pr_f[:], in_=pr_bf[:])
-            pt = psum.tile([P, 512], F32, name="pt", tag="t", bufs=3)
+            pt = psum.tile([P, 512], F32, name="pt", tag="t", bufs=NT)
             nc.tensor.transpose(pt[:, 0:P], pr_f[:], ident[:])
-            prm = const.tile([P, 2 * NC], F32, name="prm")
-            nc.vector.tensor_copy(out=prm[:], in_=pt[:, 0 : 2 * NC])
+            prm = const.tile([P, 4 * NC], F32, name="prm")
+            nc.vector.tensor_copy(out=prm[:], in_=pt[:, 0 : 4 * NC])
+            lcol = const.tile([P, 2 * NC], BF16, name="lcol")
+            nc.vector.tensor_copy(out=lcol[:], in_=prm[:, 2 * NC : 4 * NC])
+            g_ps = psum.tile([P, D], BF16, name="g_ps", tag="g_ps", bufs=1)
+            b_ps = psum.tile([P, D], BF16, name="b_ps", tag="b_ps", bufs=1)
+            for c in range(NC):
+                nc.tensor.transpose(g_ps[:, c * P : (c + 1) * P], lcol[:, c : c + 1].to_broadcast([P, P]), ident_bf[:])
+                nc.tensor.transpose(b_ps[:, c * P : (c + 1) * P], lcol[:, NC + c : NC + c + 1].to_broadcast([P, P]), ident_bf[:])
             pf = const.tile([P, 1], F32, name="pf")
             nc.vector.tensor_copy(out=pf[:], in_=p_bf[:])
             nc.vector.tensor_scalar(out=sg[:], in0=pf[:], scalar1=1.0, scalar2=2.0, op0=ALU.is_le, op1=ALU.mult)
@@ -229,7 +242,7 @@ def tile_coattention_pb_kernel(tc, x, res_a, ctx_v, W_v, bn_v_g, bn_v_b, prelu_v
 
             for b in range(B):
                 for c in range(NC):
-                    y = mm(c, b, "y", 5)
+                    y = mm(c, b, "y", NY)
                     nc.vector.bn_stats(out=st[:, c, b, :], in_=y[:])
                     if b == B - 1:
                         with tc.high_priority():
@@ -263,12 +276,12 @@ def tile_coattention_pb_kernel(tc, x, res_a, ctx_v, W_v, bn_v_g, bn_v_b, prelu_v
                     if lq in G_LQ:
                         continue
                     ov = o_t[lq][:, b, :]
-                    nc.vector.scalar_tensor_tensor(out=ov, in0=ov, scalar=nms[b * NQ + lq][:, 0:1], in1=g_bc[:], op0=ALU.add, op1=ALU.mult)
+                    nc.vector.scalar_tensor_tensor(out=ov, in0=ov, scalar=nms[b * NQ + lq][:, 0:1], in1=g_ps[:], op0=ALU.add, op1=ALU.mult)
                 for lq in lqs:
                     if lq in G_LQ:
                         continue
                     ov = o_t[lq][:, b, :]
-                    nc.vector.scalar_tensor_tensor(out=ov, in0=ov, scalar=rss[b * NQ + lq][:, 0:1], in1=b_bc[:], op0=ALU.mult, op1=ALU.add)
+                    nc.vector.scalar_tensor_tensor(out=ov, in0=ov, scalar=rss[b * NQ + lq][:, 0:1], in1=b_ps[:], op0=ALU.mult, op1=ALU.add)
                 for lq in lqs:
                     ov = o_t[lq][:, b, :]
                     r = b * NQ + lq
@@ -277,7 +290,7 @@ def tile_coattention_pb_kernel(tc, x, res_a, ctx_v, W_v, bn_v_g, bn_v_b, prelu_v
 
             def mm_parts(u, j):
                 c = 4 * u[1] + j
-                y = mm(c, u[0], "t", 3)
+                y = mm(c, u[0], "t", NT)
                 parts(u[0], c, y)
 
             units = [(b, h) for b in ORDER for h in range(2)]
@@ -306,7 +319,7 @@ def tile_coattention_pb_kernel(tc, x, res_a, ctx_v, W_v, bn_v_g, bn_v_b, prelu_v
 
             pm = small.tile([P, 1], F32, name="pm", tag="pm")
             nc.vector.tensor_reduce(out=pm[:], in_=am[:], axis=AX.X, op=ALU.max)
-            tb2 = psum.tile([P, 512], F32, name="tb2", tag="t", bufs=3)
+            tb2 = psum.tile([P, 512], F32, name="tb2", tag="t", bufs=NT)
             nc.tensor.transpose(tb2[:, 0:P], pm[:, 0:1].to_broadcast([P, P]), ident[:])
             gm = small.tile([P, 1], F32, name="gm", tag="gm")
             nc.vector.tensor_reduce(out=gm[:], in_=tb2[:, 0:P], axis=AX.X, op=ALU.max)

@@ -24,11 +24,13 @@ V_CAST = 2752
 ORDER = (3, 0, 1, 2)
 PE_ADD = ((0, 0), (0, 1), (1, 0), (1, 1), (2, 0), (2, 1))
 V_EVERY = 0
-NT = 3
-NY = 3
-V_Q1 = ()
-G_LQ = (1,)
-RAMP = 2
+PS_GB = False
+NT = 3 if PS_GB else 4
+NY = 3 if PS_GB else 4
+KEPT = ORDER[:2]
+V_STAT = ()
+G_APPLY = ()
+S_PAIRS = ((2, 0),)
 
 
 def tile_coattention_pb_kernel(tc, x, res_a, ctx_v, W_v, bn_v_g, bn_v_b, prelu_v, ln_g, ln_b, out_0, out_1):
@@ -41,7 +43,7 @@ def tile_coattention_pb_kernel(tc, x, res_a, ctx_v, W_v, bn_v_g, bn_v_b, prelu_v
         const = es.enter_context(tc.tile_pool(name="const", bufs=1))
         small = es.enter_context(tc.tile_pool(name="small", bufs=4))
         keep = es.enter_context(tc.tile_pool(name="keep", bufs=1))
-        qp = es.enter_context(tc.tile_pool(name="q", bufs=2))
+        qp = es.enter_context(tc.tile_pool(name="q", bufs=4))
         psum = es.enter_context(tc.psum_pool(name="psum", bufs=2))
 
         eps_t = const.tile([P, 1], F32, name="eps_t")
@@ -104,16 +106,14 @@ def tile_coattention_pb_kernel(tc, x, res_a, ctx_v, W_v, bn_v_g, bn_v_b, prelu_v
             return y
 
         def parts(b, c, y):
-            if c == 0:
-                q1 = qp.tile([P, NC, L], F32, name="q1", tag="q1")
-                q2 = qp.tile([P, NC, L], F32, name="q2", tag="q2")
-                q1s[b] = q1
-                q2s[b] = q2
-            nc.scalar.activation(out=q2s[b][:, c, :], in_=y[:], func=ACT.Relu, scale=sc4[:, c, 1:2], bias=bi[:, c, 1:2])
-            if c in V_Q1:
-                nc.vector.tensor_scalar(out=q1s[b][:, c, :], in0=y[:], scalar1=sc4[:, c, 0:1], scalar2=bi[:, c, 0:1], op0=ALU.mult, op1=ALU.add)
-            else:
-                nc.scalar.activation(out=q1s[b][:, c, :], in_=y[:], func=ACT.Identity, scale=sc4[:, c, 0:1], bias=bi[:, c, 0:1])
+            u = (b, c // 4)
+            if c % 4 == 0:
+                q1 = qp.tile([P, 4, L], F32, name="q1", tag="q1")
+                q2 = qp.tile([P, 4, L], F32, name="q2", tag="q2")
+                q1s[u] = q1
+                q2s[u] = q2
+            nc.scalar.activation(out=q2s[u][:, c % 4, :], in_=y[:], func=ACT.Relu, scale=sc4[:, c, 1:2], bias=bi[:, c, 1:2])
+            nc.scalar.activation(out=q1s[u][:, c % 4, :], in_=y[:], func=ACT.Identity, scale=sc4[:, c, 0:1], bias=bi[:, c, 0:1])
 
         def back(b, h, lq):
             t = psum.tile([P, 512], F32, name="t", tag="y", bufs=NY)
@@ -122,15 +122,15 @@ def tile_coattention_pb_kernel(tc, x, res_a, ctx_v, W_v, bn_v_g, bn_v_b, prelu_v
                 for i in range(2):
                     nc.tensor.matmul(out=t[:], lhsT=si_bf[:], rhs=streams[(b, lq)][i][:, h * 512 : (h + 1) * 512], start=(i == 0), stop=False)
             for j in range(4):
-                c = 4 * h + j
-                nc.tensor.matmul(out=t[:, j * P : (j + 1) * P], lhsT=q1s[b][:, c, lq * P : (lq + 1) * P], rhs=ident[:], is_transpose=True, start=not on_pe, stop=False)
-                nc.tensor.matmul(out=t[:, j * P : (j + 1) * P], lhsT=q2s[b][:, c, lq * P : (lq + 1) * P], rhs=ident[:], is_transpose=True, start=False, stop=(j == 3 or not on_pe))
+                nc.tensor.matmul(out=t[:, j * P : (j + 1) * P], lhsT=q1s[(b, h)][:, j, lq * P : (lq + 1) * P], rhs=ident[:], is_transpose=True, start=not on_pe, stop=False)
+                nc.tensor.matmul(out=t[:, j * P : (j + 1) * P], lhsT=q2s[(b, h)][:, j, lq * P : (lq + 1) * P], rhs=ident[:], is_transpose=True, start=False, stop=(j == 3 or not on_pe))
             ov = o_t[lq][:, b, h * 512 : (h + 1) * 512]
             r = b * NQ + lq
+            acc = None if (b, lq) in V_STAT else sums[:, r, h : h + 1]
             if on_pe:
-                nc.scalar.activation(out=ov, in_=t[:], func=ACT.Copy, scale=sg[:, 0:1], accum_out=sums[:, r, h : h + 1])
+                nc.scalar.activation(out=ov, in_=t[:], func=ACT.Copy, scale=sg[:, 0:1], accum_out=acc)
             else:
-                nc.vector.scalar_tensor_tensor(out=ov, in0=t[:], scalar=sg[:, 0:1], in1=ov, op0=ALU.mult, op1=ALU.add, accum_out=sums[:, r, h : h + 1])
+                nc.vector.scalar_tensor_tensor(out=ov, in0=t[:], scalar=sg[:, 0:1], in1=ov, op0=ALU.mult, op1=ALU.add, accum_out=acc)
 
         def add_streams(b):
             for lq in range(NQ):
@@ -182,7 +182,7 @@ def tile_coattention_pb_kernel(tc, x, res_a, ctx_v, W_v, bn_v_g, bn_v_b, prelu_v
                         in_=gr[:, g, :],
                     )
 
-            jobs = [("w", c) for c in range(NC)] + [("c", i) for i in range(B * NQ)]
+            jobs = [("w", c) for c in range(NC)] + [("c", b * NQ + i) for b in ORDER[2:] + KEPT for i in range(NQ)]
             for key in jobs[:8]:
                 load(key)
 
@@ -194,11 +194,14 @@ def tile_coattention_pb_kernel(tc, x, res_a, ctx_v, W_v, bn_v_g, bn_v_b, prelu_v
             nc.vector.tensor_copy(out=prm[:], in_=pt[:, 0 : 4 * NC])
             lcol = const.tile([P, 2 * NC], BF16, name="lcol")
             nc.vector.tensor_copy(out=lcol[:], in_=prm[:, 2 * NC : 4 * NC])
-            g_ps = psum.tile([P, D], BF16, name="g_ps", tag="g_ps", bufs=1)
-            b_ps = psum.tile([P, D], BF16, name="b_ps", tag="b_ps", bufs=1)
-            for c in range(NC):
-                nc.tensor.transpose(g_ps[:, c * P : (c + 1) * P], lcol[:, c : c + 1].to_broadcast([P, P]), ident_bf[:])
-                nc.tensor.transpose(b_ps[:, c * P : (c + 1) * P], lcol[:, NC + c : NC + c + 1].to_broadcast([P, P]), ident_bf[:])
+            if PS_GB:
+                g_ps = psum.tile([P, D], BF16, name="g_ps", tag="g_ps", bufs=1)
+                b_ps = psum.tile([P, D], BF16, name="b_ps", tag="b_ps", bufs=1)
+                for c in range(NC):
+                    nc.tensor.transpose(g_ps[:, c * P : (c + 1) * P], lcol[:, c : c + 1].to_broadcast([P, P]), ident_bf[:])
+                    nc.tensor.transpose(b_ps[:, c * P : (c + 1) * P], lcol[:, NC + c : NC + c + 1].to_broadcast([P, P]), ident_bf[:])
+                pools["g"] = g_ps
+                pools["b"] = b_ps
             pf = const.tile([P, 1], F32, name="pf")
             nc.vector.tensor_copy(out=pf[:], in_=p_bf[:])
             nc.vector.tensor_scalar(out=sg[:], in0=pf[:], scalar1=1.0, scalar2=2.0, op0=ALU.is_le, op1=ALU.mult)
@@ -228,6 +231,8 @@ def tile_coattention_pb_kernel(tc, x, res_a, ctx_v, W_v, bn_v_g, bn_v_b, prelu_v
             pools["late"] = late
             g_bc = late.tile([P, D], BF16, name="g_bc", bufs=1)
             b_bc = late.tile([P, D], BF16, name="b_bc", bufs=1)
+            g_v = pools.get("g", g_bc)
+            b_v = pools.get("b", b_bc)
             for b in ORDER:
                 add_streams(b)
                 if b == ORDER[0]:
@@ -240,16 +245,21 @@ def tile_coattention_pb_kernel(tc, x, res_a, ctx_v, W_v, bn_v_g, bn_v_b, prelu_v
                 nc.sync.dma_start(out=ra[:], in_=res_a[b, lq * P : (lq + 1) * P, :])
                 streams[(b, lq)] = (xa, ra)
 
-            for b in range(B):
-                for c in range(NC):
-                    y = mm(c, b, "y", NY)
+            for c in range(NC):
+                ys = {}
+                for b in ORDER[2:] + KEPT:
+                    if b in KEPT:
+                        y = mm(c, b, "t", NT)
+                    else:
+                        y = mm(c, b, "y", NY)
                     nc.vector.bn_stats(out=st[:, c, b, :], in_=y[:])
-                    if b == B - 1:
-                        with tc.high_priority():
-                            chain(c)
-                        parts(b, c, y)
-                        if c >= 4:
-                            back(b, 0, c - 4)
+                    ys[b] = y
+                with tc.high_priority():
+                    chain(c)
+                for b in KEPT:
+                    parts(b, c, ys[b])
+                if c >= 4:
+                    back(KEPT[0], 0, c - 4)
 
             def ln_stats(b, lq):
                 r = b * NQ + lq
@@ -265,23 +275,59 @@ def tile_coattention_pb_kernel(tc, x, res_a, ctx_v, W_v, bn_v_g, bn_v_b, prelu_v
                 nms[r] = nm
                 rss[r] = rs2
 
+            def ln_stats_v(b, lq):
+                r = b * NQ + lq
+                lst = small.tile([P, 2, 6], F32, name="lst", tag="lst")
+                for h in range(2):
+                    nc.vector.bn_stats(out=lst[:, h, :], in_=o_t[lq][:, b, h * 512 : (h + 1) * 512])
+                mv2 = small.tile([P, 2], F32, name="mv2", tag="mv2", bufs=8)
+                nc.vector.bn_aggr(out=mv2[:], in_=lst[:].rearrange("p h s -> p (h s)"))
+                rs2 = small.tile([P, 1], F32, name="rs2", tag="rs2", bufs=8)
+                nc.scalar.activation(out=rs2[:], in_=mv2[:, 1:2], func=ACT.Abs_reciprocal_sqrt, bias=eps_t[:, 0:1], scale=1.0)
+                nms[r] = mv2
+                rss[r] = rs2
+
             def g_apply(b, lq):
                 ov = o_t[lq][:, b, :]
                 nc.gpsimd.tensor_scalar(out=ov, in0=ov, scalar1=nms[b * NQ + lq][:, 0:1], scalar2=rss[b * NQ + lq][:, 0:1], op0=ALU.add, op1=ALU.mult)
                 nc.gpsimd.tensor_tensor(out=ov, in0=ov, in1=g_bc[:], op=ALU.mult)
                 nc.gpsimd.tensor_tensor(out=ov, in0=ov, in1=b_bc[:], op=ALU.add)
 
+            def s_apply(b, l0):
+                f = qp.tile([P, NC, 2 * P], F32, name="f", tag="q1")
+                for lq in (l0, l0 + 1):
+                    r = b * NQ + lq
+                    ov = o_t[lq][:, b, :]
+                    nb = small.tile([P, 1], F32, name="nb", tag="nb")
+                    nc.scalar.activation(out=nb[:], in_=nms[r][:, 0:1], func=ACT.Copy, scale=rss[r][:, 0:1])
+                    nc.scalar.activation(out=ov, in_=ov, func=ACT.Identity, scale=rss[r][:, 0:1], bias=nb[:, 0:1])
+                for cp in range(NC // 2):
+                    bank = psum.tile([P, 512], F32, name="nt", tag="t", bufs=NT)
+                    for e in range(2):
+                        c = 2 * cp + e
+                        for i in range(2):
+                            nc.tensor.transpose(bank[:, (2 * e + i) * P : (2 * e + i + 1) * P], o_t[l0 + i][:, b, c * P : (c + 1) * P], ident[:])
+                    for e in range(2):
+                        c = 2 * cp + e
+                        nc.scalar.activation(out=f[:, c, :], in_=bank[:, 2 * e * P : (2 * e + 2) * P], func=ACT.Identity, scale=prm[:, 2 * NC + c : 2 * NC + c + 1], bias=prm[:, 3 * NC + c : 3 * NC + c + 1])
+                for i in range(2):
+                    for h in range(2):
+                        bank = psum.tile([P, 512], F32, name="ft", tag="y", bufs=NY)
+                        for j in range(4):
+                            nc.tensor.transpose(bank[:, j * P : (j + 1) * P], f[:, 4 * h + j, i * P : (i + 1) * P], ident[:])
+                        nc.scalar.copy(out=o_t[l0 + i][:, b, h * 512 : (h + 1) * 512], in_=bank[:])
+
             def ln_apply(b, lqs):
                 for lq in lqs:
-                    if lq in G_LQ:
+                    if (b, lq) in G_APPLY or (b, lq) in S_PAIRS or (b, lq - 1) in S_PAIRS:
                         continue
                     ov = o_t[lq][:, b, :]
-                    nc.vector.scalar_tensor_tensor(out=ov, in0=ov, scalar=nms[b * NQ + lq][:, 0:1], in1=g_ps[:], op0=ALU.add, op1=ALU.mult)
+                    nc.vector.scalar_tensor_tensor(out=ov, in0=ov, scalar=nms[b * NQ + lq][:, 0:1], in1=g_v[:], op0=(ALU.subtract if (b, lq) in V_STAT else ALU.add), op1=ALU.mult)
                 for lq in lqs:
-                    if lq in G_LQ:
+                    if (b, lq) in G_APPLY or (b, lq) in S_PAIRS or (b, lq - 1) in S_PAIRS:
                         continue
                     ov = o_t[lq][:, b, :]
-                    nc.vector.scalar_tensor_tensor(out=ov, in0=ov, scalar=rss[b * NQ + lq][:, 0:1], in1=b_ps[:], op0=ALU.mult, op1=ALU.add)
+                    nc.vector.scalar_tensor_tensor(out=ov, in0=ov, scalar=rss[b * NQ + lq][:, 0:1], in1=b_v[:], op0=ALU.mult, op1=ALU.add)
                 for lq in lqs:
                     ov = o_t[lq][:, b, :]
                     r = b * NQ + lq
@@ -293,29 +339,36 @@ def tile_coattention_pb_kernel(tc, x, res_a, ctx_v, W_v, bn_v_g, bn_v_b, prelu_v
                 y = mm(c, u[0], "t", NT)
                 parts(u[0], c, y)
 
-            units = [(b, h) for b in ORDER for h in range(2)]
-            NU = len(units)
-            for n in range(2, NU + 2):
-                first = RAMP if n == 2 else 4
+            up = [(b, h) for b in ORDER[2:] for h in range(2)]
+            down = [(b, h) for b in ORDER for h in range(2)][1:]
+            rest = []
+            for i in range(len(down)):
+                b, h = down[i]
                 for j in range(4):
-                    if n < NU and j < first:
-                        mm_parts(units[n], j)
-                    if n - 1 < NU:
-                        back(units[n - 1][0], units[n - 1][1], j)
-                if n % 2 == 0:
+                    if i < len(up):
+                        mm_parts(up[i], j)
+                    back(b, h, j)
+                if h == 1:
+                    on_g = [lq for lq in range(NQ) if (b, lq) in G_APPLY or (b, lq) in S_PAIRS or (b, lq - 1) in S_PAIRS]
+                    on_v = [lq for lq in range(NQ) if lq not in on_g]
                     with tc.high_priority():
-                        for lq in G_LQ:
-                            ln_stats(units[n - 2][0], lq)
-                            g_apply(units[n - 2][0], lq)
                         for lq in range(NQ):
-                            if lq not in G_LQ:
-                                ln_stats(units[n - 2][0], lq)
-                for j in range(first, 4):
-                    mm_parts(units[n], j)
-                if n % 2 == 0:
-                    ln_apply(units[n - 2][0], (0, 1))
+                            if (b, lq) in V_STAT:
+                                ln_stats_v(b, lq)
+                            else:
+                                ln_stats(b, lq)
+                            if (b, lq) in G_APPLY:
+                                g_apply(b, lq)
+                            if (b, lq - 1) in S_PAIRS:
+                                s_apply(b, lq - 1)
+                    ln_apply(b, on_v[:2])
+                    rest.append((b, on_v[2:] + on_g))
                 else:
-                    ln_apply(units[n - 3][0], (2, 3))
+                    for br, lqs in rest:
+                        ln_apply(br, lqs)
+                    rest.clear()
+            for br, lqs in rest:
+                ln_apply(br, lqs)
 
             pm = small.tile([P, 1], F32, name="pm", tag="pm")
             nc.vector.tensor_reduce(out=pm[:], in_=am[:], axis=AX.X, op=ALU.max)

@@ -24,13 +24,13 @@ V_CAST = 2752
 ORDER = (3, 0, 1, 2)
 PE_ADD = ((0, 0), (0, 1), (1, 0), (1, 1), (2, 0), (2, 1))
 V_EVERY = 0
-PS_GB = False
-NT = 3 if PS_GB else 4
-NY = 3 if PS_GB else 4
+PS_GB = True
+NT = 4
+NY = 4
 KEPT = ORDER[:2]
-V_STAT = ()
-G_APPLY = ()
-S_PAIRS = ((2, 0),)
+V_STAT = tuple((b, lq) for b in ORDER for lq in (2, 3))
+G_APPLY = tuple((b, lq) for b in ORDER[:-1] for lq in (0, 1))
+S_PAIRS = ((ORDER[-1], 0),)
 
 
 def tile_coattention_pb_kernel(tc, x, res_a, ctx_v, W_v, bn_v_g, bn_v_b, prelu_v, ln_g, ln_b, out_0, out_1):
@@ -194,14 +194,6 @@ def tile_coattention_pb_kernel(tc, x, res_a, ctx_v, W_v, bn_v_g, bn_v_b, prelu_v
             nc.vector.tensor_copy(out=prm[:], in_=pt[:, 0 : 4 * NC])
             lcol = const.tile([P, 2 * NC], BF16, name="lcol")
             nc.vector.tensor_copy(out=lcol[:], in_=prm[:, 2 * NC : 4 * NC])
-            if PS_GB:
-                g_ps = psum.tile([P, D], BF16, name="g_ps", tag="g_ps", bufs=1)
-                b_ps = psum.tile([P, D], BF16, name="b_ps", tag="b_ps", bufs=1)
-                for c in range(NC):
-                    nc.tensor.transpose(g_ps[:, c * P : (c + 1) * P], lcol[:, c : c + 1].to_broadcast([P, P]), ident_bf[:])
-                    nc.tensor.transpose(b_ps[:, c * P : (c + 1) * P], lcol[:, NC + c : NC + c + 1].to_broadcast([P, P]), ident_bf[:])
-                pools["g"] = g_ps
-                pools["b"] = b_ps
             pf = const.tile([P, 1], F32, name="pf")
             nc.vector.tensor_copy(out=pf[:], in_=p_bf[:])
             nc.vector.tensor_scalar(out=sg[:], in0=pf[:], scalar1=1.0, scalar2=2.0, op0=ALU.is_le, op1=ALU.mult)
@@ -231,8 +223,6 @@ def tile_coattention_pb_kernel(tc, x, res_a, ctx_v, W_v, bn_v_g, bn_v_b, prelu_v
             pools["late"] = late
             g_bc = late.tile([P, D], BF16, name="g_bc", bufs=1)
             b_bc = late.tile([P, D], BF16, name="b_bc", bufs=1)
-            g_v = pools.get("g", g_bc)
-            b_v = pools.get("b", b_bc)
             for b in ORDER:
                 add_streams(b)
                 if b == ORDER[0]:
@@ -260,6 +250,15 @@ def tile_coattention_pb_kernel(tc, x, res_a, ctx_v, W_v, bn_v_g, bn_v_b, prelu_v
                     parts(b, c, ys[b])
                 if c >= 4:
                     back(KEPT[0], 0, c - 4)
+
+            g_v = g_bc
+            b_v = b_bc
+            if PS_GB:
+                g_v = psum.tile([P, D], BF16, name="g_ps", tag="t", bufs=NT)
+                b_v = psum.tile([P, D], BF16, name="b_ps", tag="t", bufs=NT)
+                for c in range(NC):
+                    nc.tensor.transpose(g_v[:, c * P : (c + 1) * P], lcol[:, c : c + 1].to_broadcast([P, P]), ident_bf[:])
+                    nc.tensor.transpose(b_v[:, c * P : (c + 1) * P], lcol[:, NC + c : NC + c + 1].to_broadcast([P, P]), ident_bf[:])
 
             def ln_stats(b, lq):
                 r = b * NQ + lq
@@ -351,16 +350,15 @@ def tile_coattention_pb_kernel(tc, x, res_a, ctx_v, W_v, bn_v_g, bn_v_b, prelu_v
                 if h == 1:
                     on_g = [lq for lq in range(NQ) if (b, lq) in G_APPLY or (b, lq) in S_PAIRS or (b, lq - 1) in S_PAIRS]
                     on_v = [lq for lq in range(NQ) if lq not in on_g]
-                    with tc.high_priority():
-                        for lq in range(NQ):
-                            if (b, lq) in V_STAT:
-                                ln_stats_v(b, lq)
-                            else:
-                                ln_stats(b, lq)
-                            if (b, lq) in G_APPLY:
-                                g_apply(b, lq)
-                            if (b, lq - 1) in S_PAIRS:
-                                s_apply(b, lq - 1)
+                    for lq in range(NQ):
+                        if (b, lq) in V_STAT:
+                            ln_stats_v(b, lq)
+                        else:
+                            ln_stats(b, lq)
+                        if (b, lq) in G_APPLY:
+                            g_apply(b, lq)
+                        if (b, lq - 1) in S_PAIRS:
+                            s_apply(b, lq - 1)
                     ln_apply(b, on_v[:2])
                     rest.append((b, on_v[2:] + on_g))
                 else:

@@ -90,6 +90,8 @@ def tile_coattention_pb_kernel(tc, x, res_a, ctx_v, W_v, bn_v_g, bn_v_b, prelu_v
         streams = {}
         nms = {}
         rss = {}
+        mvs = {}
+        lsts = {}
 
         def mm(c, b, tag, bufs):
             y = psum.tile([P, 512], F32, name="y", tag=tag, bufs=bufs)
@@ -143,8 +145,7 @@ def tile_coattention_pb_kernel(tc, x, res_a, ctx_v, W_v, bn_v_g, bn_v_b, prelu_v
                 nc.gpsimd.tensor_tensor(out=o_t[lq][:, b, :], in0=xt[:], in1=rt[:], op=ALU.add)
 
         def chain(c):
-            mv = small.tile([P, 2], F32, name="mv", tag="mv")
-            nc.vector.bn_aggr(out=mv[:], in_=st[:, c, :, :].rearrange("p b s -> p (b s)"))
+            mv = mvs[c]
             rs = small.tile([P, 1], F32, name="rs", tag="rs")
             nc.scalar.activation(out=rs[:], in_=mv[:, 1:2], func=ACT.Abs_reciprocal_sqrt, bias=eps_t[:, 0:1], scale=1.0)
             nc.scalar.activation(out=sc4[:, c, :], in_=g4[:, c, :], func=ACT.Copy, scale=rs[:, 0:1])
@@ -235,6 +236,18 @@ def tile_coattention_pb_kernel(tc, x, res_a, ctx_v, W_v, bn_v_g, bn_v_b, prelu_v
                 nc.sync.dma_start(out=ra[:], in_=res_a[b, lq * P : (lq + 1) * P, :])
                 streams[(b, lq)] = (xa, ra)
 
+            def finish(c, ys):
+                mv = small.tile([P, 2], F32, name="mv", tag="mv")
+                nc.vector.bn_aggr(out=mv[:], in_=st[:, c, :, :].rearrange("p b s -> p (b s)"))
+                mvs[c] = mv
+                with tc.high_priority():
+                    chain(c)
+                for b in KEPT:
+                    parts(b, c, ys[b])
+                if c >= 4:
+                    back(KEPT[0], 0, c - 4)
+
+            before = None
             for c in range(NC):
                 ys = {}
                 for b in ORDER[2:] + KEPT:
@@ -244,12 +257,10 @@ def tile_coattention_pb_kernel(tc, x, res_a, ctx_v, W_v, bn_v_g, bn_v_b, prelu_v
                         y = mm(c, b, "y", NY)
                     nc.vector.bn_stats(out=st[:, c, b, :], in_=y[:])
                     ys[b] = y
-                with tc.high_priority():
-                    chain(c)
-                for b in KEPT:
-                    parts(b, c, ys[b])
-                if c >= 4:
-                    back(KEPT[0], 0, c - 4)
+                    if b == ORDER[2] and c > 0:
+                        finish(c - 1, before)
+                before = ys
+            finish(NC - 1, before)
 
             g_v = g_bc
             b_v = b_bc
@@ -276,9 +287,7 @@ def tile_coattention_pb_kernel(tc, x, res_a, ctx_v, W_v, bn_v_g, bn_v_b, prelu_v
 
             def ln_stats_v(b, lq):
                 r = b * NQ + lq
-                lst = small.tile([P, 2, 6], F32, name="lst", tag="lst")
-                for h in range(2):
-                    nc.vector.bn_stats(out=lst[:, h, :], in_=o_t[lq][:, b, h * 512 : (h + 1) * 512])
+                lst = lsts[r]
                 mv2 = small.tile([P, 2], F32, name="mv2", tag="mv2", bufs=8)
                 nc.vector.bn_aggr(out=mv2[:], in_=lst[:].rearrange("p h s -> p (h s)"))
                 rs2 = small.tile([P, 1], F32, name="rs2", tag="rs2", bufs=8)
@@ -352,6 +361,12 @@ def tile_coattention_pb_kernel(tc, x, res_a, ctx_v, W_v, bn_v_g, bn_v_b, prelu_v
                     on_v = [lq for lq in range(NQ) if lq not in on_g]
                     for lq in range(NQ):
                         if (b, lq) in V_STAT:
+                            lst = small.tile([P, 2, 6], F32, name="lst", tag="lst")
+                            for hh in range(2):
+                                nc.vector.bn_stats(out=lst[:, hh, :], in_=o_t[lq][:, b, hh * 512 : (hh + 1) * 512])
+                            lsts[b * NQ + lq] = lst
+                    for lq in range(NQ):
+                        if (b, lq) in V_STAT:
                             ln_stats_v(b, lq)
                         else:
                             ln_stats(b, lq)
@@ -369,15 +384,14 @@ def tile_coattention_pb_kernel(tc, x, res_a, ctx_v, W_v, bn_v_g, bn_v_b, prelu_v
                 ln_apply(br, lqs)
 
             pm = small.tile([P, 1], F32, name="pm", tag="pm")
-            nc.vector.tensor_reduce(out=pm[:], in_=am[:], axis=AX.X, op=ALU.max)
+            am_s = small.tile([P, NQ * B], F32, name="am_s", tag="am_s")
+            nc.vector.tensor_scalar(out=am_s[:], in0=am[:], scalar1=1.0 / 448.0, scalar2=None, op0=ALU.mult, op1=ALU.max, accum_out=pm[:])
             tb2 = psum.tile([P, 512], F32, name="tb2", tag="t", bufs=NT)
             nc.tensor.transpose(tb2[:, 0:P], pm[:, 0:1].to_broadcast([P, P]), ident[:])
             gm = small.tile([P, 1], F32, name="gm", tag="gm")
             nc.vector.tensor_reduce(out=gm[:], in_=tb2[:, 0:P], axis=AX.X, op=ALU.max)
-            ri = small.tile([P, 1], F32, name="ri", tag="ri")
-            nc.vector.reciprocal(out=ri[:], in_=gm[:])
             fac = small.tile([P, 1], F32, name="fac", tag="fac")
-            nc.vector.tensor_scalar(out=fac[:], in0=ri[:], scalar1=448.0, scalar2=None, op0=ALU.mult)
+            nc.vector.reciprocal(out=fac[:], in_=gm[:])
             for lq in range(NQ):
                 of = o_t[lq][:].rearrange("p b d -> p (b d)")
                 f8 = late.tile([P, B * D], FP8, name="f8", tag="f8", bufs=4)

@@ -28,8 +28,9 @@ PS_GB = True
 NT = 4
 NY = 4
 KEPT = ORDER[:2]
-V_STAT = tuple((b, lq) for b in ORDER for lq in (2, 3))
-G_APPLY = tuple((b, lq) for b in ORDER[:-1] for lq in (0, 1))
+PIN = 5
+V_STAT = tuple((b, lq) for b in ORDER for lq in (2, 3) if (b, lq) != (ORDER[2], 2))
+G_APPLY = tuple((b, lq) for b in ORDER[:-1] for lq in (0, 1)) + ((ORDER[2], 2),)
 S_PAIRS = ((ORDER[-1], 0),)
 
 
@@ -350,7 +351,8 @@ def tile_coattention_pb_kernel(tc, x, res_a, ctx_v, W_v, bn_v_g, bn_v_b, prelu_v
             up = [(b, h) for b in ORDER[2:] for h in range(2)]
             down = [(b, h) for b in ORDER for h in range(2)][1:]
             rest = []
-            for i in range(len(down)):
+            held = []
+            def unit(i):
                 b, h = down[i]
                 for j in range(4):
                     if i < len(up):
@@ -375,14 +377,19 @@ def tile_coattention_pb_kernel(tc, x, res_a, ctx_v, W_v, bn_v_g, bn_v_b, prelu_v
                         if (b, lq - 1) in S_PAIRS:
                             s_apply(b, lq - 1)
                     ln_apply(b, on_v[:2])
-                    rest.append((b, on_v[2:] + on_g))
+                    (held if b == ORDER[2] else rest).append((b, on_v[2:] + on_g))
                 else:
                     for br, lqs in rest:
                         ln_apply(br, lqs)
                     rest.clear()
-            for br, lqs in rest:
-                ln_apply(br, lqs)
 
+            for i in range(PIN):
+                unit(i)
+            with tc.manual_schedule(engines={mybir.EngineType.DVE}):
+                for i in range(PIN, len(down)):
+                    unit(i)
+                for br, lqs in held + rest:
+                    ln_apply(br, lqs)
             pm = small.tile([P, 1], F32, name="pm", tag="pm")
             am_s = small.tile([P, NQ * B], F32, name="am_s", tag="am_s")
             nc.vector.tensor_scalar(out=am_s[:], in0=am[:], scalar1=1.0 / 448.0, scalar2=None, op0=ALU.mult, op1=ALU.max, accum_out=pm[:])

@@ -382,13 +382,17 @@ def tile_coattention_pb_kernel(tc, x, res_a, ctx_v, W_v, bn_v_g, bn_v_b, prelu_v
                     for br, lqs in rest:
                         ln_apply(br, lqs)
                     rest.clear()
+                    for br, lqs in held:
+                        ln_apply(br, lqs[0:1])
 
             for i in range(PIN):
                 unit(i)
             with tc.manual_schedule(engines={mybir.EngineType.DVE}):
                 for i in range(PIN, len(down)):
                     unit(i)
-                for br, lqs in held + rest:
+                for br, lqs in held:
+                    ln_apply(br, lqs[1:])
+                for br, lqs in rest:
                     ln_apply(br, lqs)
             pm = small.tile([P, 1], F32, name="pm", tag="pm")
             am_s = small.tile([P, NQ * B], F32, name="am_s", tag="am_s")

@@ -28,6 +28,7 @@ PS_GB = True
 NT = 4
 NY = 4
 KEPT = ORDER[:2]
+KEPT_U = ((3, 0), (3, 1), (0, 0))
 PIN = 5
 V_STAT = tuple((b, lq) for b in ORDER for lq in (2, 3) if (b, lq) != (ORDER[2], 2))
 G_APPLY = tuple((b, lq) for b in ORDER[:-1] for lq in (0, 1)) + ((ORDER[2], 2),)
@@ -244,15 +245,14 @@ def tile_coattention_pb_kernel(tc, x, res_a, ctx_v, W_v, bn_v_g, bn_v_b, prelu_v
                 with tc.high_priority():
                     chain(c)
                 for b in KEPT:
-                    parts(b, c, ys[b])
-                if c >= 4:
-                    back(KEPT[0], 0, c - 4)
+                    if (b, c // 4) in KEPT_U:
+                        parts(b, c, ys[b])
 
             before = None
             for c in range(NC):
                 ys = {}
                 for b in ORDER[2:] + KEPT:
-                    if b in KEPT:
+                    if (b, c // 4) in KEPT_U:
                         y = mm(c, b, "t", NT)
                     else:
                         y = mm(c, b, "y", NY)
@@ -262,6 +262,8 @@ def tile_coattention_pb_kernel(tc, x, res_a, ctx_v, W_v, bn_v_g, bn_v_b, prelu_v
                         finish(c - 1, before)
                 before = ys
             finish(NC - 1, before)
+            for lq in range(NQ):
+                back(KEPT[0], 0, lq)
 
             g_v = g_bc
             b_v = b_bc
@@ -348,7 +350,7 @@ def tile_coattention_pb_kernel(tc, x, res_a, ctx_v, W_v, bn_v_g, bn_v_b, prelu_v
                 y = mm(c, u[0], "t", NT)
                 parts(u[0], c, y)
 
-            up = [(b, h) for b in ORDER[2:] for h in range(2)]
+            up = [(b, h) for b in ORDER for h in range(2) if (b, h) not in KEPT_U]
             down = [(b, h) for b in ORDER for h in range(2)][1:]
             rest = []
             held = []

from contextlib import ExitStack

import concourse.mybir as mybir
from concourse.masks import make_identity

L, B, D = 512, 4, 1024
P = 128
NC = D // P
NQ = L // P
EPS = 1e-5
FLOPS = 2 * B * L * D * D

F32 = mybir.dt.float32
BF16 = mybir.dt.bfloat16
U32 = mybir.dt.uint32
U8 = mybir.dt.uint8
FP8X4 = mybir.dt.float8_e4m3fn_x4
FP8 = mybir.dt.float8_e4m3fn
ALU = mybir.AluOpType
ACT = mybir.ActivationFunctionType
AX = mybir.AxisListType

V_CAST = 2752
ORDER = (3, 0, 1, 2)
PE_ADD = ((0, 0), (0, 1), (1, 0), (1, 1), (2, 0), (2, 1))
V_EVERY = 0
PS_GB = True
NT = 4
NY = 4
KEPT = ORDER[:2]
KEPT_U = ((3, 0), (3, 1), (0, 0))
PIN = 5
V_STAT = tuple((b, lq) for b in ORDER for lq in (2, 3) if (b, lq) != (ORDER[2], 2))
G_APPLY = tuple((b, lq) for b in ORDER[:-1] for lq in (0, 1)) + ((ORDER[2], 2),)
S_PAIRS = ((ORDER[-1], 0),)


def tile_coattention_pb_kernel(tc, x, res_a, ctx_v, W_v, bn_v_g, bn_v_b, prelu_v, ln_g, ln_b, out_0, out_1):
    nc = tc.nc
    ctx_rows = ctx_v.flatten_outer_dims()
    out0_rows = out_0.rearrange("l b d -> l (b d)")
    out1_rows = out_1.rearrange("l b d -> l (b d)")

    with ExitStack() as es:
        const = es.enter_context(tc.tile_pool(name="const", bufs=1))
        small = es.enter_context(tc.tile_pool(name="small", bufs=4))
        keep = es.enter_context(tc.tile_pool(name="keep", bufs=1))
        qp = es.enter_context(tc.tile_pool(name="q", bufs=4))
        psum = es.enter_context(tc.psum_pool(name="psum", bufs=2))

        eps_t = const.tile([P, 1], F32, name="eps_t")
        nc.vector.memset(eps_t[:], EPS)
        zero_t = const.tile([P, 1], F32, name="zero_t")
        nc.vector.memset(zero_t[:], 0.0)
        warm = const.tile([P, 1], F32, name="warm")
        nc.scalar.activation(out=warm[:], in_=eps_t[:], func=ACT.Abs_reciprocal_sqrt)
        ident = const.tile([P, P], F32, name="ident")
        make_identity(nc, ident[:])

        pr_bf = const.tile([P, P], BF16, name="pr_bf")
        nc.vector.memset(pr_bf[:], 0.0)
        nc.sync.dma_start(out=pr_bf[0:NC, :], in_=bn_v_g.rearrange("(c p) -> c p", p=P))
        nc.sync.dma_start(out=pr_bf[NC : 2 * NC, :], in_=bn_v_b.rearrange("(c p) -> c p", p=P))
        nc.sync.dma_start(out=pr_bf[2 * NC : 3 * NC, :], in_=ln_g.rearrange("(c p) -> c p", p=P))
        nc.sync.dma_start(out=pr_bf[3 * NC : 4 * NC, :], in_=ln_b.rearrange("(c p) -> c p", p=P))
        ident_bf = const.tile([P, P], BF16, name="ident_bf")
        make_identity(nc, ident_bf[:])
        p_bf = const.tile([P, 1], BF16, name="p_bf")
        nc.sync.dma_start(out=p_bf[:], in_=prelu_v.partition_broadcast(P))

        o_t = []
        for lq in range(NQ):
            o_lq = keep.tile([P, B, D], F32, name="o%d" % lq)
            o_t.append(o_lq)
        cc = keep.tile([P, 2, B * L], U32, name="cc", align_bytes=64)
        cs = keep.tile([P, 2, B * L], U8, name="cs", align_bytes=64)
        wc = keep.tile([P, 2, D], U32, name="wc", align_bytes=64)
        ws = keep.tile([P, 2, D], U8, name="ws", align_bytes=64)
        st = const.tile([P, NC, B, 6], F32, name="st")
        sc4 = const.tile([P, NC, 4], F32, name="sc4")
        bi = const.tile([P, NC, 2], F32, name="bi")
        sums = const.tile([P, NQ * B, 2], F32, name="sums")
        am = const.tile([P, NQ * B], F32, name="am")
        g4 = const.tile([P, NC, 4], F32, name="g4")
        kb = const.tile([P, NC, 2], F32, name="kb")
        sg = const.tile([P, 1], F32, name="sg")
        si_bf = const.tile([P, P], BF16, name="si_bf")

        pools = {}
        q1s = {}
        q2s = {}
        streams = {}
        nms = {}
        rss = {}
        mvs = {}
        lsts = {}

        def mm(c, b, tag, bufs):
            y = psum.tile([P, 512], F32, name="y", tag=tag, bufs=bufs)
            for g in range(2):
                nc.tensor.matmul_mx(
                    out=y[:],
                    lhsT=wc[:, g, c * P : (c + 1) * P].bitcast(FP8X4),
                    lhsT_scale=ws[:, g, c * P : (c + 1) * P],
                    rhs=cc[:, g, b * L : (b + 1) * L].bitcast(FP8X4),
                    rhs_scale=cs[:, g, b * L : (b + 1) * L],
                    start=(g == 0),
                    stop=(g == 1),
                )
            return y

        def parts(b, c, y):
            u = (b, c // 4)
            if c % 4 == 0:
                q1 = qp.tile([P, 4, L], F32, name="q1", tag="q1")
                q2 = qp.tile([P, 4, L], F32, name="q2", tag="q2")
                q1s[u] = q1
                q2s[u] = q2
            nc.scalar.activation(out=q2s[u][:, c % 4, :], in_=y[:], func=ACT.Relu, scale=sc4[:, c, 1:2], bias=bi[:, c, 1:2])
            nc.scalar.activation(out=q1s[u][:, c % 4, :], in_=y[:], func=ACT.Identity, scale=sc4[:, c, 0:1], bias=bi[:, c, 0:1])

        def back(b, h, lq):
            t = psum.tile([P, 512], F32, name="t", tag="y", bufs=NY)
            on_pe = (b, lq) in PE_ADD
            if on_pe:
                for i in range(2):
                    nc.tensor.matmul(out=t[:], lhsT=si_bf[:], rhs=streams[(b, lq)][i][:, h * 512 : (h + 1) * 512], start=(i == 0), stop=False)
            for j in range(4):
                nc.tensor.matmul(out=t[:, j * P : (j + 1) * P], lhsT=q1s[(b, h)][:, j, lq * P : (lq + 1) * P], rhs=ident[:], is_transpose=True, start=not on_pe, stop=False)
                nc.tensor.matmul(out=t[:, j * P : (j + 1) * P], lhsT=q2s[(b, h)][:, j, lq * P : (lq + 1) * P], rhs=ident[:], is_transpose=True, start=False, stop=(j == 3 or not on_pe))
            ov = o_t[lq][:, b, h * 512 : (h + 1) * 512]
            r = b * NQ + lq
            acc = None if (b, lq) in V_STAT else sums[:, r, h : h + 1]
            if on_pe:
                nc.scalar.activation(out=ov, in_=t[:], func=ACT.Copy, scale=sg[:, 0:1], accum_out=acc)
            else:
                nc.vector.scalar_tensor_tensor(out=ov, in0=t[:], scalar=sg[:, 0:1], in1=ov, op0=ALU.mult, op1=ALU.add, accum_out=acc)

        def add_streams(b):
            for lq in range(NQ):
                if (b, lq) in PE_ADD:
                    continue
                xt = pools["late"].tile([P, D], BF16, name="xt", tag="xt", bufs=4)
                nc.sync.dma_start(out=xt[:], in_=x[lq * P : (lq + 1) * P, b, :])
                rt = pools["late"].tile([P, D], BF16, name="rt", tag="rt", bufs=4)
                nc.sync.dma_start(out=rt[:], in_=res_a[b, lq * P : (lq + 1) * P, :])
                nc.gpsimd.tensor_tensor(out=o_t[lq][:, b, :], in0=xt[:], in1=rt[:], op=ALU.add)

        def chain(c):
            mv = mvs[c]
            rs = small.tile([P, 1], F32, name="rs", tag="rs")
            nc.scalar.activation(out=rs[:], in_=mv[:, 1:2], func=ACT.Abs_reciprocal_sqrt, bias=eps_t[:, 0:1], scale=1.0)
            nc.scalar.activation(out=sc4[:, c, :], in_=g4[:, c, :], func=ACT.Copy, scale=rs[:, 0:1])
            for i in range(2):
                nc.scalar.activation(out=bi[:, c, i : i + 1], in_=sc4[:, c, 2 + i : 3 + i], func=ACT.Identity, scale=mv[:, 0:1], bias=kb[:, c, i : i + 1])

        with tc.tile_pool(name="stage", bufs=2) as stage:
            raws = {}

            def load(key):
                raw = stage.tile([P, D], BF16, name="raw", tag="raw", bufs=8)
                nc.sync.dma_start(out=raw[:], in_=(W_v if key[0] == "w" else ctx_rows)[key[1] * P : (key[1] + 1) * P, :])
                raws[key] = raw

            def turn(key, dst, on_vector):
                words = raws[key][:].bitcast(F32)
                bank = psum.tile([P, 512], F32, name="tb", tag="t", bufs=NT)
                for g in range(2):
                    for u in range(2):
                        j = 2 * g + u
                        nc.tensor.transpose(bank[:, j * P : (j + 1) * P], words[:, 256 * g + u : 256 * (g + 1) : 2], ident[:])
                src = bank[:].rearrange("p (g u r) -> p g r u", g=2, u=2)
                if on_vector:
                    nc.vector.tensor_copy(out=dst, in_=src)
                else:
                    nc.scalar.copy(out=dst, in_=src)

            def quant(key, gr):
                codes_t, scales_t = (wc, ws) if key[0] == "w" else (cc, cs)
                col = key[1] * P
                for g in range(2):
                    nc.vector.quantize_mx(
                        out=codes_t[:, g, col : col + 4 * P].bitcast(FP8X4),
                        scales=scales_t[:, g, col : col + 4 * P],
                        in_=gr[:, g, :],
                    )

            jobs = [("w", c) for c in range(NC)] + [("c", b * NQ + i) for b in ORDER[2:] + KEPT for i in range(NQ)]
            for key in jobs[:8]:
                load(key)

            pr_f = const.tile([P, P], F32, name="pr_f")
            nc.vector.tensor_copy(out=pr_f[:], in_=pr_bf[:])
            pt = psum.tile([P, 512], F32, name="pt", tag="t", bufs=NT)
            nc.tensor.transpose(pt[:, 0:P], pr_f[:], ident[:])
            prm = const.tile([P, 4 * NC], F32, name="prm")
            nc.vector.tensor_copy(out=prm[:], in_=pt[:, 0 : 4 * NC])
            lcol = const.tile([P, 2 * NC], BF16, name="lcol")
            nc.vector.tensor_copy(out=lcol[:], in_=prm[:, 2 * NC : 4 * NC])
            pf = const.tile([P, 1], F32, name="pf")
            nc.vector.tensor_copy(out=pf[:], in_=p_bf[:])
            nc.vector.tensor_scalar(out=sg[:], in0=pf[:], scalar1=1.0, scalar2=2.0, op0=ALU.is_le, op1=ALU.mult)
            nc.vector.tensor_scalar(out=sg[:], in0=sg[:], scalar1=-1.0, scalar2=None, op0=ALU.add)
            nc.vector.tensor_scalar(out=si_bf[:], in0=ident[:], scalar1=sg[:, 0:1], scalar2=None, op0=ALU.mult)
            k4 = const.tile([P, 4], F32, name="k4")
            nc.vector.tensor_tensor(out=k4[:, 0:1], in0=sg[:], in1=pf[:], op=ALU.mult)
            nc.vector.tensor_tensor(out=k4[:, 1:2], in0=sg[:], in1=k4[:, 0:1], op=ALU.subtract)
            nc.vector.tensor_scalar(out=k4[:, 2:4], in0=k4[:, 0:2], scalar1=-1.0, scalar2=None, op0=ALU.mult)
            for c in range(NC):
                nc.gpsimd.tensor_scalar(out=g4[:, c, :], in0=k4[:], scalar1=prm[:, c : c + 1], scalar2=None, op0=ALU.mult)
                nc.gpsimd.tensor_scalar(out=kb[:, c, :], in0=k4[:, 0:2], scalar1=prm[:, NC + c : NC + c + 1], scalar2=None, op0=ALU.mult)

            def do_group(i0):
                gr = stage.tile([P, 2, 16 * P], BF16, name="gr", tag="gr", bufs=2, align_bytes=64)
                grv = gr[:].bitcast(F32).rearrange("p g (r u) -> p g r u", u=2)
                for i in range(i0, i0 + 4):
                    if i + 8 < len(jobs):
                        load(jobs[i + 8])
                    turn(jobs[i], grv[:, :, (i - i0) * P : (i - i0 + 1) * P, :], V_EVERY > 0 and i % V_EVERY == V_EVERY - 1)
                quant(jobs[i0], gr)

            for i0 in range(0, len(jobs), 4):
                do_group(i0)

        with tc.tile_pool(name="late", bufs=2) as late:
            pools["late"] = late
            g_bc = late.tile([P, D], BF16, name="g_bc", bufs=1)
            b_bc = late.tile([P, D], BF16, name="b_bc", bufs=1)
            for b in ORDER:
                add_streams(b)
                if b == ORDER[0]:
                    nc.sync.dma_start(out=g_bc[:], in_=ln_g.partition_broadcast(P))
                    nc.sync.dma_start(out=b_bc[:], in_=ln_b.partition_broadcast(P))
            for b, lq in PE_ADD:
                xa = late.tile([P, D], BF16, name="xa%d%d" % (b, lq), bufs=1)
                nc.sync.dma_start(out=xa[:], in_=x[lq * P : (lq + 1) * P, b, :])
                ra = late.tile([P, D], BF16, name="ra%d%d" % (b, lq), bufs=1)
                nc.sync.dma_start(out=ra[:], in_=res_a[b, lq * P : (lq + 1) * P, :])
                streams[(b, lq)] = (xa, ra)

            def finish(c, ys):
                mv = small.tile([P, 2], F32, name="mv", tag="mv")
                nc.vector.bn_aggr(out=mv[:], in_=st[:, c, :, :].rearrange("p b s -> p (b s)"))
                mvs[c] = mv
                with tc.high_priority():
                    chain(c)
                for b in KEPT:
                    if (b, c // 4) in KEPT_U:
                        parts(b, c, ys[b])

            before = None
            for c in range(NC):
                ys = {}
                for b in ORDER[2:] + KEPT:
                    if (b, c // 4) in KEPT_U:
                        y = mm(c, b, "t", NT)
                    else:
                        y = mm(c, b, "y", NY)
                    nc.vector.bn_stats(out=st[:, c, b, :], in_=y[:])
                    ys[b] = y
                    if b == ORDER[2] and c > 0:
                        finish(c - 1, before)
                before = ys
            finish(NC - 1, before)
            for lq in range(NQ):
                back(KEPT[0], 0, lq)

            g_v = g_bc
            b_v = b_bc
            if PS_GB:
                g_v = psum.tile([P, D], BF16, name="g_ps", tag="t", bufs=NT)
                b_v = psum.tile([P, D], BF16, name="b_ps", tag="t", bufs=NT)
                for c in range(NC):
                    nc.tensor.transpose(g_v[:, c * P : (c + 1) * P], lcol[:, c : c + 1].to_broadcast([P, P]), ident_bf[:])
                    nc.tensor.transpose(b_v[:, c * P : (c + 1) * P], lcol[:, NC + c : NC + c + 1].to_broadcast([P, P]), ident_bf[:])

            def ln_stats(b, lq):
                r = b * NQ + lq
                ov = o_t[lq][:, b, :]
                j2 = small.tile([P, 2], F32, name="j2", tag="j2")
                nm = small.tile([P, 1], F32, name="nm", tag="nm", bufs=8)
                nc.scalar.activation(out=j2[:], in_=sums[:, r, :], func=ACT.Copy, scale=-1.0 / D, accum_out=nm[:])
                junk = late.tile([P, D], BF16, name="junk", tag="junk")
                ss = small.tile([P, 1], F32, name="ss", tag="ss")
                nc.scalar.activation(out=junk[:], in_=ov, func=ACT.Square, bias=nm[:, 0:1], scale=1.0, accum_out=ss[:])
                rs2 = small.tile([P, 1], F32, name="rs2", tag="rs2", bufs=8)
                nc.scalar.activation(out=rs2[:], in_=ss[:], func=ACT.Abs_reciprocal_sqrt, bias=eps_t[:, 0:1], scale=1.0 / D)
                nms[r] = nm
                rss[r] = rs2

            def ln_stats_v(b, lq):
                r = b * NQ + lq
                lst = lsts[r]
                mv2 = small.tile([P, 2], F32, name="mv2", tag="mv2", bufs=8)
                nc.vector.bn_aggr(out=mv2[:], in_=lst[:].rearrange("p h s -> p (h s)"))
                rs2 = small.tile([P, 1], F32, name="rs2", tag="rs2", bufs=8)
                nc.scalar.activation(out=rs2[:], in_=mv2[:, 1:2], func=ACT.Abs_reciprocal_sqrt, bias=eps_t[:, 0:1], scale=1.0)
                nms[r] = mv2
                rss[r] = rs2

            def g_apply(b, lq):
                ov = o_t[lq][:, b, :]
                nc.gpsimd.tensor_scalar(out=ov, in0=ov, scalar1=nms[b * NQ + lq][:, 0:1], scalar2=rss[b * NQ + lq][:, 0:1], op0=ALU.add, op1=ALU.mult)
                nc.gpsimd.tensor_tensor(out=ov, in0=ov, in1=g_bc[:], op=ALU.mult)
                nc.gpsimd.tensor_tensor(out=ov, in0=ov, in1=b_bc[:], op=ALU.add)

            def s_apply(b, l0):
                f = qp.tile([P, NC, 2 * P], F32, name="f", tag="q1")
                for lq in (l0, l0 + 1):
                    r = b * NQ + lq
                    ov = o_t[lq][:, b, :]
                    nb = small.tile([P, 1], F32, name="nb", tag="nb")
                    nc.scalar.activation(out=nb[:], in_=nms[r][:, 0:1], func=ACT.Copy, scale=rss[r][:, 0:1])
                    nc.scalar.activation(out=ov, in_=ov, func=ACT.Identity, scale=rss[r][:, 0:1], bias=nb[:, 0:1])
                for cp in range(NC // 2):
                    bank = psum.tile([P, 512], F32, name="nt", tag="t", bufs=NT)
                    for e in range(2):
                        c = 2 * cp + e
                        for i in range(2):
                            nc.tensor.transpose(bank[:, (2 * e + i) * P : (2 * e + i + 1) * P], o_t[l0 + i][:, b, c * P : (c + 1) * P], ident[:])
                    for e in range(2):
                        c = 2 * cp + e
                        nc.scalar.activation(out=f[:, c, :], in_=bank[:, 2 * e * P : (2 * e + 2) * P], func=ACT.Identity, scale=prm[:, 2 * NC + c : 2 * NC + c + 1], bias=prm[:, 3 * NC + c : 3 * NC + c + 1])
                for i in range(2):
                    for h in range(2):
                        bank = psum.tile([P, 512], F32, name="ft", tag="y", bufs=NY)
                        for j in range(4):
                            nc.tensor.transpose(bank[:, j * P : (j + 1) * P], f[:, 4 * h + j, i * P : (i + 1) * P], ident[:])
                        nc.scalar.copy(out=o_t[l0 + i][:, b, h * 512 : (h + 1) * 512], in_=bank[:])

            def ln_apply(b, lqs):
                for lq in lqs:
                    if (b, lq) in G_APPLY or (b, lq) in S_PAIRS or (b, lq - 1) in S_PAIRS:
                        continue
                    ov = o_t[lq][:, b, :]
                    nc.vector.scalar_tensor_tensor(out=ov, in0=ov, scalar=nms[b * NQ + lq][:, 0:1], in1=g_v[:], op0=(ALU.subtract if (b, lq) in V_STAT else ALU.add), op1=ALU.mult)
                for lq in lqs:
                    if (b, lq) in G_APPLY or (b, lq) in S_PAIRS or (b, lq - 1) in S_PAIRS:
                        continue
                    ov = o_t[lq][:, b, :]
                    nc.vector.scalar_tensor_tensor(out=ov, in0=ov, scalar=rss[b * NQ + lq][:, 0:1], in1=b_v[:], op0=ALU.mult, op1=ALU.add)
                for lq in lqs:
                    ov = o_t[lq][:, b, :]
                    r = b * NQ + lq
                    nc.vector.tensor_reduce(out=am[:, r : r + 1], in_=ov, axis=AX.X, op=ALU.max, apply_absolute_value=True)
                    nc.sync.dma_start(out=out0_rows[lq * P : (lq + 1) * P, b * D : (b + 1) * D], in_=ov)

            def mm_parts(u, j):
                c = 4 * u[1] + j
                y = mm(c, u[0], "t", NT)
                parts(u[0], c, y)

            up = [(b, h) for b in ORDER for h in range(2) if (b, h) not in KEPT_U]
            down = [(b, h) for b in ORDER for h in range(2)][1:]
            rest = []
            held = []
            def unit(i):
                b, h = down[i]
                for j in range(4):
                    if i < len(up):
                        mm_parts(up[i], j)
                    back(b, h, j)
                if h == 1:
                    on_g = [lq for lq in range(NQ) if (b, lq) in G_APPLY or (b, lq) in S_PAIRS or (b, lq - 1) in S_PAIRS]
                    on_v = [lq for lq in range(NQ) if lq not in on_g]
                    for lq in range(NQ):
                        if (b, lq) in V_STAT:
                            lst = small.tile([P, 2, 6], F32, name="lst", tag="lst")
                            for hh in range(2):
                                nc.vector.bn_stats(out=lst[:, hh, :], in_=o_t[lq][:, b, hh * 512 : (hh + 1) * 512])
                            lsts[b * NQ + lq] = lst
                    for lq in range(NQ):
                        if (b, lq) in V_STAT:
                            ln_stats_v(b, lq)
                        else:
                            ln_stats(b, lq)
                        if (b, lq) in G_APPLY:
                            g_apply(b, lq)
                        if (b, lq - 1) in S_PAIRS:
                            s_apply(b, lq - 1)
                    ln_apply(b, on_v[:2])
                    (held if b == ORDER[2] else rest).append((b, on_v[2:] + on_g))
                else:
                    for br, lqs in rest:
                        ln_apply(br, lqs)
                    rest.clear()
                    for br, lqs in held:
                        ln_apply(br, lqs[0:1])

            for i in range(PIN):
                unit(i)
            with tc.manual_schedule(engines={mybir.EngineType.DVE}):
                for i in range(PIN, len(down)):
                    unit(i)
                for br, lqs in held:
                    ln_apply(br, lqs[1:])
                for br, lqs in rest:
                    ln_apply(br, lqs)
            pm = small.tile([P, 1], F32, name="pm", tag="pm")
            am_s = small.tile([P, NQ * B], F32, name="am_s", tag="am_s")
            nc.vector.tensor_scalar(out=am_s[:], in0=am[:], scalar1=1.0 / 448.0, scalar2=None, op0=ALU.mult, op1=ALU.max, accum_out=pm[:])
            tb2 = psum.tile([P, 512], F32, name="tb2", tag="t", bufs=NT)
            nc.tensor.transpose(tb2[:, 0:P], pm[:, 0:1].to_broadcast([P, P]), ident[:])
            gm = small.tile([P, 1], F32, name="gm", tag="gm")
            nc.vector.tensor_reduce(out=gm[:], in_=tb2[:, 0:P], axis=AX.X, op=ALU.max)
            fac = small.tile([P, 1], F32, name="fac", tag="fac")
            nc.vector.reciprocal(out=fac[:], in_=gm[:])
            for lq in range(NQ):
                of = o_t[lq][:].rearrange("p b d -> p (b d)")
                f8 = late.tile([P, B * D], FP8, name="f8", tag="f8", bufs=4)
                if lq < NQ - 1:
                    cuts = ((0, V_CAST, B * D),)
                else:
                    cuts = ((0, V_CAST // 2, B * D // 2), (B * D // 2, B * D // 2 + V_CAST // 2, B * D))
                for lo, mid, hi in cuts:
                    nc.vector.tensor_scalar(out=f8[:, lo:mid], in0=of[:, lo:mid], scalar1=fac[:, 0:1], scalar2=None, op0=ALU.mult, saturate=False)
                    nc.scalar.activation(out=f8[:, mid:hi], in_=of[:, mid:hi], func=ACT.Identity, scale=fac[:, 0:1], bias=zero_t[:, 0:1], saturate=False)
                    nc.sync.dma_start(out=out1_rows[lq * P : (lq + 1) * P, lo:hi], in_=f8[:, lo:hi].bitcast(U8))
